import numpy as np
import ml_dtypes


def mxq(x, axis, fmt="e4m3"):
    dtype, down = {"e4m3": (ml_dtypes.float8_e4m3fn, 7), "e5m2": (ml_dtypes.float8_e5m2, 14)}[fmt]
    v = np.moveaxis(np.asarray(x, np.float32).astype(ml_dtypes.bfloat16).astype(np.float64), axis, -1)
    blocks = v.reshape(v.shape[:-1] + (-1, 32))
    amax = np.abs(blocks).max(-1, keepdims=True)
    byte = np.maximum(np.where(amax > 0, np.frexp(amax)[1] - 1 + 127, 0) - down, 1)
    scale = np.exp2(byte - 127.0)
    codes = (blocks / scale).astype(np.float32).astype(dtype).astype(np.float64)
    return np.moveaxis((codes * scale).reshape(v.shape), -1, axis)


WIDE = False


def mx_kscale(k):
    if not WIDE:
        return np.ones(k)
    levels = np.array([10, -10, 5, -5, 0])
    a = np.random.permutation(np.resize(levels, k // 512 * 4)).reshape(k // 512, 4)
    idx = np.arange(k)
    return np.exp2(a[idx // 512, idx % 128 // 32])


BF16 = ml_dtypes.bfloat16


def bf(x):
    return np.asarray(x, np.float32).astype(BF16)


def f64(x):
    return np.asarray(x).astype(np.float64)


B, S, D, K, O, DEG, BLK = 4, 1024, 1024, 1024, 512, 4, 512
HALF = DEG // 2
STEP = K // DEG
KH = HALF * STEP


def make_masks(lo, hi):
    rows = np.arange(K)
    deg_r = (rows * DEG) // K + 1
    degmask = (np.arange(1, DEG + 1)[:, None] <= deg_r[None, :]) * 1.0
    tri_l = np.tril(np.ones((K, D)))
    tri_u = np.triu(np.ones((K, D)))
    return np.stack([degmask[i][:, None] * (tri_l if i % 2 == 0 else tri_u) for i in range(lo, hi)])


def factor(zq, Wi, i):
    y = np.zeros((zq.shape[0], K))
    for j in range(K // BLK):
        a, b = max(j * BLK, i * STEP), (j + 1) * BLK
        c0, c1 = (0, min(b, D)) if i % 2 == 0 else (j * BLK, D)
        if a >= b or c0 >= c1:
            continue
        y[:, a:b] = zq[:, c0:c1] @ mxq(Wi[a - KH:b - KH, c0:c1], 1, "e4m3").T
    return y


def setup_inputs():
    s, t = mx_kscale(D), mx_kscale(K)
    return {"z": bf(np.random.standard_normal((B, S, D)) * s),
            "chain_lo": bf(np.random.standard_normal((B * S, K)) * t),
            "U_hi": bf(np.random.standard_normal((DEG - HALF, K - KH, D)) / np.sqrt(D) / s),
            "masks_hi": bf(make_masks(HALF, DEG)[:, KH:, :]),
            "C_w": bf(np.random.standard_normal((O, K)) / np.sqrt(K) / t),
            "C_b": bf(np.random.standard_normal(O) * 0.5)}


def reference(z, chain_lo, U_hi, masks_hi, C_w, C_b):
    lead = z.shape[:-1]
    zq = mxq(f64(z).reshape(-1, D), 1, "e4m3")
    W = f64(masks_hi) * f64(U_hi)
    out = f64(chain_lo)
    for i in range(HALF, DEG):
        out = factor(zq, W[i - HALF], i) * out + out
    x = (mxq(out, 1, "e4m3") @ mxq(f64(C_w), 1, "e4m3").T) + f64(C_b)
    return x.reshape(*lead, O)

@@ -1,0 +1,301 @@
+from contextlib import ExitStack
+
+import concourse.mybir as mybir
+from concourse.masks import make_identity
+
+F32 = mybir.dt.float32
+BF16 = mybir.dt.bfloat16
+U32 = mybir.dt.uint32
+U8 = mybir.dt.uint8
+FP8X4 = mybir.dt.float8_e4m3fn_x4
+ADD = mybir.AluOpType.add
+MULT = mybir.AluOpType.mult
+
+P = 128
+TOKENS = 4096
+D = 1024
+K = 1024
+O = 512
+CHUNK = 512
+NCH = TOKENS // CHUNK
+NB = 2 * NCH
+LAG = 2
+ZBUFS = 5
+CBUFS = 5
+
+FLOPS = 2 * TOKENS * (512 * 1024 + 256 * 512 + 1024 * 512)
+BYTES = 3 * TOKENS * 1024 * 2 + 2 * (512 * 1024 + 256 * 512) * 2 + O * K * 2 + O * 2
+
+
+def tile_cp_sparse_degree_lu_pb_t_kernel(tc, z, chain_lo, U_hi, masks_hi, C_w, C_b, out):
+    nc = tc.nc
+    zf = z.flatten_outer_dims()
+    xf = out.flatten_outer_dims()
+
+    with ExitStack() as ctx:
+        keep = ctx.enter_context(tc.tile_pool(name="keep", bufs=1))
+        stream = ctx.enter_context(tc.tile_pool(name="stream", bufs=2))
+        pst = ctx.enter_context(tc.psum_pool(name="pst", bufs=1))
+        psm = ctx.enter_context(tc.psum_pool(name="psm", bufs=4))
+        ctx.enter_context(tc.manual_schedule())
+
+        ident_f = keep.tile([P, P], F32, name="ident_f")
+        ident_b = keep.tile([P, P], BF16, name="ident_b")
+        make_identity(nc, ident_f[:])
+        make_identity(nc, ident_b[:])
+        ones = keep.tile([P, P], BF16, name="ones")
+        brow = keep.tile([P, O], BF16, name="brow")
+        bias = keep.tile([P, O], F32, name="bias")
+        nc.vector.memset(ones[:], 1.0)
+        nc.vector.memset(brow[:], 0.0)
+
+        un = keep.tile([P, 4 * D], BF16, name="un")
+        mn = keep.tile([P, 4 * D], BF16, name="mn")
+        u3 = keep.tile([P, 2 * 512], BF16, name="u3")
+        m3 = keep.tile([P, 2 * 512], BF16, name="m3")
+        cwn = keep.tile([P, 4 * K], BF16, name="cwn")
+        w2g = keep.tile([P, 2 * 512 * 4], BF16, name="w2g", align_bytes=64)
+        w3g = keep.tile([P, 256 * 4], BF16, name="w3g", align_bytes=64)
+        cwg = keep.tile([P, 2 * 512 * 4], BF16, name="cwg", align_bytes=64)
+        w2c = keep.tile([P, 2 * 512], U32, name="w2c", align_bytes=64)
+        w2s = keep.tile([P, 2 * 512], U8, name="w2s", align_bytes=64)
+        w3c = keep.tile([P, 256], U32, name="w3c", align_bytes=64)
+        w3s = keep.tile([P, 256], U8, name="w3s", align_bytes=64)
+        cwc = keep.tile([P, 2 * 512], U32, name="cwc", align_bytes=64)
+        cws = keep.tile([P, 2 * 512], U8, name="cws", align_bytes=64)
+
+        zn = {}
+        cn = {}
+
+        def rows(ap2d, ch):
+            return ap2d[ch * CHUNK:(ch + 1) * CHUNK, :].rearrange("(p j) c -> p j c", j=4)
+
+        def load_z(ch, halves=1):
+            zn[ch] = stream.tile([P, 4 * D], BF16, name="zn", tag="zn", bufs=ZBUFS)
+            dst = zn[ch][:].rearrange("p (j c) -> p j c", j=4)
+            src = rows(zf, ch)
+            step = 4 // halves
+            for h in range(halves):
+                nc.sync.dma_start(out=dst[:, h * step:(h + 1) * step, :], in_=src[:, h * step:(h + 1) * step, :])
+
+        def load_c(ch):
+            cn[ch] = stream.tile([P, 4 * K], BF16, name="cn", tag="cn", bufs=CBUFS)
+            nc.sync.dma_start(out=cn[ch][:].rearrange("p (j c) -> p j c", j=4), in_=rows(chain_lo, ch))
+
+        zn[0] = stream.tile([P, 4 * D], BF16, name="zn", tag="zn", bufs=ZBUFS)
+        z0dst = zn[0][:].rearrange("p (j c) -> p j c", j=4)
+        nc.sync.dma_start(out=z0dst[:, 0:2, :], in_=rows(zf, 0)[:, 0:2, :])
+        u_src = U_hi[0].rearrange("(t p) c -> p t c", p=P)
+        m_src = masks_hi[0].rearrange("(t p) c -> p t c", p=P)
+        u_dst = un[:].rearrange("p (t c) -> p t c", t=4)
+        m_dst = mn[:].rearrange("p (t c) -> p t c", t=4)
+        for h in range(2):
+            nc.sync.dma_start(out=u_dst[:, 2 * h:2 * h + 2, :], in_=u_src[:, 2 * h:2 * h + 2, :])
+            nc.sync.dma_start(out=m_dst[:, 2 * h:2 * h + 2, :], in_=m_src[:, 2 * h:2 * h + 2, :])
+        nc.sync.dma_start(out=z0dst[:, 2:4, :], in_=rows(zf, 0)[:, 2:4, :])
+        nc.sync.dma_start(out=u3[:].rearrange("p (t c) -> p t c", t=2),
+                          in_=U_hi[1, 256:512, 512:1024].rearrange("(t p) c -> p t c", p=P))
+        nc.sync.dma_start(out=m3[:].rearrange("p (t c) -> p t c", t=2),
+                          in_=masks_hi[1, 256:512, 512:1024].rearrange("(t p) c -> p t c", p=P))
+        load_c(0)
+        load_z(1)
+        nc.sync.dma_start(out=cwn[:].rearrange("p (t c) -> p t c", t=4),
+                          in_=C_w.rearrange("(t p) c -> p t c", p=P))
+        nc.sync.dma_start(out=brow[0:1, :], in_=C_b.unsqueeze(0))
+        load_c(1)
+        for ch in range(2, ZBUFS):
+            load_z(ch)
+            load_c(ch)
+
+        def prep_w23():
+            unw = un[:].bitcast(F32)
+            w2gw = w2g[:].bitcast(F32).rearrange("p (g r u) -> p g r u", g=2, u=2)
+            for h in range(2):
+                for tl in range(2):
+                    t = 2 * h + tl
+                    nc.vector.tensor_tensor(out=un[:, t * D:(t + 1) * D], in0=un[:, t * D:(t + 1) * D],
+                                            in1=mn[:, t * D:(t + 1) * D], op=MULT)
+                for g in range(2):
+                    bank = pst.tile([P, 512], F32, name="tw", tag="tz", bufs=2)
+                    for u in range(2):
+                        for tl in range(2):
+                            t = 2 * h + tl
+                            w0 = t * 512 + 256 * g + 128 * u
+                            nc.tensor.transpose(bank[:, 256 * u + 128 * tl:256 * u + 128 * tl + 128],
+                                                unw[:, w0:w0 + 128], ident_f[:])
+                    nc.vector.tensor_copy(out=w2gw[:, g, 256 * h:256 * h + 256, :],
+                                          in_=bank[:].rearrange("p (u r) -> p r u", u=2))
+            nc.vector.tensor_tensor(out=u3[:], in0=u3[:], in1=m3[:], op=MULT)
+            for g in range(2):
+                nc.vector.quantize_mx(out=w2c[:, 512 * g:512 * g + 512].bitcast(FP8X4),
+                                      scales=w2s[:, 512 * g:512 * g + 512],
+                                      in_=w2g[:, 2048 * g:2048 * g + 2048])
+            u3w = u3[:].bitcast(F32)
+            bank = pst.tile([P, 512], F32, name="tw", tag="tz", bufs=2)
+            for u in range(2):
+                for tl in range(2):
+                    w0 = tl * 256 + 128 * u
+                    nc.tensor.transpose(bank[:, 256 * u + 128 * tl:256 * u + 128 * tl + 128],
+                                        u3w[:, w0:w0 + 128], ident_f[:])
+            nc.vector.tensor_copy(out=w3g[:].bitcast(F32).rearrange("p (r u) -> p r u", u=2),
+                                  in_=bank[:].rearrange("p (u r) -> p r u", u=2))
+            nc.vector.quantize_mx(out=w3c[:].bitcast(FP8X4), scales=w3s[:], in_=w3g[:])
+
+        def prep_cw():
+            cww = cwn[:].bitcast(F32)
+            cwgw = cwg[:].bitcast(F32).rearrange("p (g r u) -> p g r u", g=2, u=2)
+            cwgb = cwg[:].rearrange("p (g r t) -> p g r t", g=2, t=4)
+            for h in range(2):
+                bank = pst.tile([P, 512], F32, name="tw", tag="tz", bufs=2)
+                for u in range(2):
+                    for tl in range(2):
+                        w0 = (2 * h + tl) * 512 + 128 * u
+                        nc.tensor.transpose(bank[:, 256 * u + 128 * tl:256 * u + 128 * tl + 128],
+                                            cww[:, w0:w0 + 128], ident_f[:])
+                nc.vector.tensor_copy(out=cwgw[:, 0, 256 * h:256 * h + 256, :],
+                                      in_=bank[:].rearrange("p (u r) -> p r u", u=2))
+            for h in range(2):
+                bankb = pst.tile([P, 1024], BF16, name="twb", tag="toh", bufs=1)
+                for t in range(4):
+                    for tl in range(2):
+                        c0 = (2 * h + tl) * K + 512 + 128 * t
+                        nc.tensor.transpose(bankb[:, 256 * t + 128 * tl:256 * t + 128 * tl + 128],
+                                            cwn[:, c0:c0 + 128], ident_b[:])
+                nc.vector.tensor_copy(out=cwgb[:, 1, 256 * h:256 * h + 256, :],
+                                      in_=bankb[:].rearrange("p (t r) -> p r t", t=4))
+            for g in range(2):
+                nc.vector.quantize_mx(out=cwc[:, 512 * g:512 * g + 512].bitcast(FP8X4),
+                                      scales=cws[:, 512 * g:512 * g + 512],
+                                      in_=cwg[:, 2048 * g:2048 * g + 2048])
+            bb = pst.tile([P, 512], F32, name="tbias", tag="tcl", bufs=1)
+            nc.tensor.matmul(out=bb[:], lhsT=ones[:], rhs=brow[:], start=True, stop=True)
+            nc.vector.tensor_copy(out=bias[:], in_=bb[:])
+
+        zg = {}
+        zc = {}
+        zs = {}
+        y2 = {}
+        y3 = {}
+        oh = {}
+        og = {}
+        oc = {}
+        os_ = {}
+        xp = {}
+
+        def t_z(b):
+            ch, h = divmod(b, 2)
+            zw = zn[ch][:].bitcast(F32)
+            zg[b] = stream.tile([P, 2048], BF16, name="zg", tag="zg", bufs=2, align_bytes=64)
+            zgw = zg[b][:].bitcast(F32).rearrange("p (s g r u) -> p s g r u", s=2, g=2, u=2)
+            for s in range(2):
+                j = 2 * h + s
+                bank = pst.tile([P, 512], F32, name="tz", tag="tz", bufs=2)
+                for gu in range(4):
+                    nc.tensor.transpose(bank[:, 128 * gu:128 * gu + 128],
+                                        zw[:, 512 * j + 128 * gu:512 * j + 128 * gu + 128], ident_f[:])
+                nc.scalar.copy(out=zgw[:, s], in_=bank[:].rearrange("p (g u r) -> p g r u", g=2, u=2))
+
+        def q_z(b):
+            zc[b] = stream.tile([P, 512], U32, name="zc", tag="zc", bufs=2, align_bytes=64)
+            zs[b] = stream.tile([P, 512], U8, name="zs", tag="zs", bufs=2, align_bytes=64)
+            nc.vector.quantize_mx(out=zc[b][:].bitcast(FP8X4), scales=zs[b][:], in_=zg[b][:])
+
+        def s_1(b):
+            y3[b] = psm.tile([P, 512], F32, name="y3", tag="mx")
+            for s in range(2):
+                y2[(b, s)] = psm.tile([P, 512], F32, name="y2", tag="mx")
+                for g in range(2):
+                    c0 = (2 * s + g) * 128
+                    nc.tensor.matmul_mx(out=y2[(b, s)][:],
+                                        lhsT=zc[b][:, c0:c0 + 128].bitcast(FP8X4), lhsT_scale=zs[b][:, c0:c0 + 128],
+                                        rhs=w2c[:, 512 * g:512 * g + 512].bitcast(FP8X4),
+                                        rhs_scale=w2s[:, 512 * g:512 * g + 512],
+                                        start=(g == 0), stop=(g == 1))
+                c0 = (2 * s + 1) * 128
+                nc.tensor.matmul_mx(out=y3[b][:, 256 * s:256 * s + 256],
+                                    lhsT=zc[b][:, c0:c0 + 128].bitcast(FP8X4), lhsT_scale=zs[b][:, c0:c0 + 128],
+                                    rhs=w3c[:].bitcast(FP8X4), rhs_scale=w3s[:],
+                                    start=True, stop=True)
+
+        def chain(b, between):
+            ch, h = divmod(b, 2)
+            oh[b] = stream.tile([P, 1024], BF16, name="oh", tag="oh", bufs=LAG + 2)
+            tmp = stream.tile([P, 512], F32, name="tmp", tag="tmp", bufs=2)
+            for s in range(2):
+                c0 = (2 * h + s) * K
+                nc.vector.scalar_tensor_tensor(out=oh[b][:, 512 * s:512 * s + 256], in0=y2[(b, s)][:, 0:256],
+                                               scalar=1.0, in1=cn[ch][:, c0 + 512:c0 + 768], op0=ADD, op1=MULT)
+                nc.vector.scalar_tensor_tensor(out=tmp[:, 256 * s:256 * s + 256], in0=y2[(b, s)][:, 256:512],
+                                               scalar=1.0, in1=cn[ch][:, c0 + 768:c0 + 1024], op0=ADD, op1=MULT)
+                if s == 0:
+                    between()
+            nc.vector.scalar_tensor_tensor(out=oh[b][:].rearrange("p (s r) -> p s r", s=2)[:, :, 256:512],
+                                           in0=y3[b][:].rearrange("p (s r) -> p s r", s=2), scalar=1.0,
+                                           in1=tmp[:].rearrange("p (s r) -> p s r", s=2), op0=ADD, op1=MULT)
+
+        def t_o(b):
+            ch, h = divmod(b, 2)
+            cw_ = cn[ch][:].bitcast(F32)
+            og[b] = stream.tile([P, 2048], BF16, name="og", tag="og", bufs=2, align_bytes=64)
+            ogw = og[b][:].bitcast(F32).rearrange("p (s g r u) -> p s g r u", s=2, g=2, u=2)
+            ogb = og[b][:].rearrange("p (s g r t) -> p s g r t", s=2, g=2, t=4)
+            bank = pst.tile([P, 512], F32, name="tcl", tag="tcl", bufs=1)
+            for s in range(2):
+                j = 2 * h + s
+                for u in range(2):
+                    nc.tensor.transpose(bank[:, 256 * s + 128 * u:256 * s + 128 * u + 128],
+                                        cw_[:, 512 * j + 128 * u:512 * j + 128 * u + 128], ident_f[:])
+            nc.scalar.copy(out=ogw[:, :, 0], in_=bank[:].rearrange("p (s u r) -> p s r u", s=2, u=2))
+            bankb = pst.tile([P, 1024], BF16, name="toh", tag="toh", bufs=1)
+            for s in range(2):
+                for t in range(4):
+                    nc.tensor.transpose(bankb[:, 512 * s + 128 * t:512 * s + 128 * t + 128],
+                                        oh[b][:, 512 * s + 128 * t:512 * s + 128 * t + 128], ident_b[:])
+            nc.scalar.copy(out=ogb[:, :, 1], in_=bankb[:].rearrange("p (s t r) -> p s r t", s=2, t=4))
+
+        def q_o(b):
+            oc[b] = stream.tile([P, 512], U32, name="oc", tag="oc", bufs=2, align_bytes=64)
+            os_[b] = stream.tile([P, 512], U8, name="os", tag="os", bufs=2, align_bytes=64)
+            nc.vector.quantize_mx(out=oc[b][:].bitcast(FP8X4), scales=os_[b][:], in_=og[b][:])
+
+        def s_2(b):
+            for s in range(2):
+                xp[(b, s)] = psm.tile([P, 512], F32, name="xp", tag="mx")
+                for g in range(2):
+                    c0 = (2 * s + g) * 128
+                    nc.tensor.matmul_mx(out=xp[(b, s)][:],
+                                        lhsT=oc[b][:, c0:c0 + 128].bitcast(FP8X4), lhsT_scale=os_[b][:, c0:c0 + 128],
+                                        rhs=cwc[:, 512 * g:512 * g + 512].bitcast(FP8X4),
+                                        rhs_scale=cws[:, 512 * g:512 * g + 512],
+                                        start=(g == 0), stop=(g == 1))
+
+        def e_x(b):
+            ch, h = divmod(b, 2)
+            xs = stream.tile([P, 1024], F32, name="xs", tag="xs", bufs=3)
+            for s in range(2):
+                nc.vector.tensor_tensor(out=xs[:, 512 * s:512 * s + 512], in0=xp[(b, s)][:], in1=bias[:], op=ADD)
+            nc.sync.dma_start(out=rows(xf, ch)[:, 2 * h:2 * h + 2, :], in_=xs[:].rearrange("p (s o) -> p s o", s=2))
+
+        for k in range(NB + LAG + 1):
+            if k < NB:
+                t_z(k)
+            if k == 0:
+                q_z(0)
+                prep_w23()
+            if 0 <= k - LAG < NB:
+                t_o(k - LAG)
+            if 0 <= k - 1 < NB:
+                s_1(k - 1)
+                chain(k - 1, (lambda: q_z(k)) if k < NB else (lambda: None))
+            if 0 <= k - LAG - 1 < NB:
+                s_2(k - LAG - 1)
+            if k == 2:
+                prep_cw()
+            if 0 <= k - LAG < NB:
+                q_o(k - LAG)
+            if 0 <= k - LAG - 1 < NB:
+                e_x(k - LAG - 1)
+            if k % 2 == 1 and (k - 1) // 2 + ZBUFS < NCH:
+                load_z((k - 1) // 2 + ZBUFS)
+            if (k - 1 - LAG) >= 0 and (k - 1 - LAG) % 2 == 0 and (k - 1 - LAG) // 2 + CBUFS < NCH:
+                load_c((k - 1 - LAG) // 2 + CBUFS)

@@ -35,8 +35,8 @@ def tile_cp_sparse_degree_lu_pb_t_kernel(tc, z, chain_lo, U_hi, masks_hi, C_w, C
     with ExitStack() as ctx:
         keep = ctx.enter_context(tc.tile_pool(name="keep", bufs=1))
         stream = ctx.enter_context(tc.tile_pool(name="stream", bufs=2))
-        pst = ctx.enter_context(tc.psum_pool(name="pst", bufs=1))
-        psm = ctx.enter_context(tc.psum_pool(name="psm", bufs=4))
+        pst = ctx.enter_context(tc.psum_pool(name="pst", bufs=3))
+        psm = ctx.enter_context(tc.psum_pool(name="psm", bufs=1))
         ctx.enter_context(tc.manual_schedule())
 
         ident_f = keep.tile([P, P], F32, name="ident_f")
@@ -116,7 +116,7 @@ def tile_cp_sparse_degree_lu_pb_t_kernel(tc, z, chain_lo, U_hi, masks_hi, C_w, C
                     nc.vector.tensor_tensor(out=un[:, t * D:(t + 1) * D], in0=un[:, t * D:(t + 1) * D],
                                             in1=mn[:, t * D:(t + 1) * D], op=MULT)
                 for g in range(2):
-                    bank = pst.tile([P, 512], F32, name="tw", tag="tz", bufs=2)
+                    bank = pst.tile([P, 512], F32, name="tw", tag="t")
                     for u in range(2):
                         for tl in range(2):
                             t = 2 * h + tl
@@ -131,7 +131,7 @@ def tile_cp_sparse_degree_lu_pb_t_kernel(tc, z, chain_lo, U_hi, masks_hi, C_w, C
                                       scales=w2s[:, 512 * g:512 * g + 512],
                                       in_=w2g[:, 2048 * g:2048 * g + 2048])
             u3w = u3[:].bitcast(F32)
-            bank = pst.tile([P, 512], F32, name="tw", tag="tz", bufs=2)
+            bank = pst.tile([P, 512], F32, name="tw", tag="t")
             for u in range(2):
                 for tl in range(2):
                     w0 = tl * 256 + 128 * u
@@ -146,7 +146,7 @@ def tile_cp_sparse_degree_lu_pb_t_kernel(tc, z, chain_lo, U_hi, masks_hi, C_w, C
             cwgw = cwg[:].bitcast(F32).rearrange("p (g r u) -> p g r u", g=2, u=2)
             cwgb = cwg[:].rearrange("p (g r t) -> p g r t", g=2, t=4)
             for h in range(2):
-                bank = pst.tile([P, 512], F32, name="tw", tag="tz", bufs=2)
+                bank = pst.tile([P, 512], F32, name="tw", tag="t")
                 for u in range(2):
                     for tl in range(2):
                         w0 = (2 * h + tl) * 512 + 128 * u
@@ -155,7 +155,7 @@ def tile_cp_sparse_degree_lu_pb_t_kernel(tc, z, chain_lo, U_hi, masks_hi, C_w, C
                 nc.vector.tensor_copy(out=cwgw[:, 0, 256 * h:256 * h + 256, :],
                                       in_=bank[:].rearrange("p (u r) -> p r u", u=2))
             for h in range(2):
-                bankb = pst.tile([P, 1024], BF16, name="twb", tag="toh", bufs=1)
+                bankb = pst.tile([P, 1024], BF16, name="twb", tag="t")
                 for t in range(4):
                     for tl in range(2):
                         c0 = (2 * h + tl) * K + 512 + 128 * t
@@ -167,7 +167,7 @@ def tile_cp_sparse_degree_lu_pb_t_kernel(tc, z, chain_lo, U_hi, masks_hi, C_w, C
                 nc.vector.quantize_mx(out=cwc[:, 512 * g:512 * g + 512].bitcast(FP8X4),
                                       scales=cws[:, 512 * g:512 * g + 512],
                                       in_=cwg[:, 2048 * g:2048 * g + 2048])
-            bb = pst.tile([P, 512], F32, name="tbias", tag="tcl", bufs=1)
+            bb = pst.tile([P, 512], F32, name="tbias", tag="t")
             nc.tensor.matmul(out=bb[:], lhsT=ones[:], rhs=brow[:], start=True, stop=True)
             nc.vector.tensor_copy(out=bias[:], in_=bb[:])
 
@@ -189,7 +189,7 @@ def tile_cp_sparse_degree_lu_pb_t_kernel(tc, z, chain_lo, U_hi, masks_hi, C_w, C
             zgw = zg[b][:].bitcast(F32).rearrange("p (s g r u) -> p s g r u", s=2, g=2, u=2)
             for s in range(2):
                 j = 2 * h + s
-                bank = pst.tile([P, 512], F32, name="tz", tag="tz", bufs=2)
+                bank = pst.tile([P, 512], F32, name="tz", tag="t")
                 for gu in range(4):
                     nc.tensor.transpose(bank[:, 128 * gu:128 * gu + 128],
                                         zw[:, 512 * j + 128 * gu:512 * j + 128 * gu + 128], ident_f[:])
@@ -201,16 +201,20 @@ def tile_cp_sparse_degree_lu_pb_t_kernel(tc, z, chain_lo, U_hi, masks_hi, C_w, C
             nc.vector.quantize_mx(out=zc[b][:].bitcast(FP8X4), scales=zs[b][:], in_=zg[b][:])
 
         def s_1(b):
-            y3[b] = psm.tile([P, 512], F32, name="y3", tag="mx")
+            y2[(b, 0)] = psm.tile([P, 512], F32, name="y2a", tag="y2a")
+            y2[(b, 1)] = psm.tile([P, 512], F32, name="y2b", tag="y2b")
+            y3[b] = psm.tile([P, 512], F32, name="y3", tag="y3")
+            for half in range(2):
+                for s in range(2):
+                    for g in range(2):
+                        c0 = (2 * s + g) * 128
+                        r0 = 512 * g + 256 * half
+                        nc.tensor.matmul_mx(out=y2[(b, half)][:, 256 * s:256 * s + 256],
+                                            lhsT=zc[b][:, c0:c0 + 128].bitcast(FP8X4),
+                                            lhsT_scale=zs[b][:, c0:c0 + 128],
+                                            rhs=w2c[:, r0:r0 + 256].bitcast(FP8X4), rhs_scale=w2s[:, r0:r0 + 256],
+                                            start=(g == 0), stop=(g == 1))
             for s in range(2):
-                y2[(b, s)] = psm.tile([P, 512], F32, name="y2", tag="mx")
-                for g in range(2):
-                    c0 = (2 * s + g) * 128
-                    nc.tensor.matmul_mx(out=y2[(b, s)][:],
-                                        lhsT=zc[b][:, c0:c0 + 128].bitcast(FP8X4), lhsT_scale=zs[b][:, c0:c0 + 128],
-                                        rhs=w2c[:, 512 * g:512 * g + 512].bitcast(FP8X4),
-                                        rhs_scale=w2s[:, 512 * g:512 * g + 512],
-                                        start=(g == 0), stop=(g == 1))
                 c0 = (2 * s + 1) * 128
                 nc.tensor.matmul_mx(out=y3[b][:, 256 * s:256 * s + 256],
                                     lhsT=zc[b][:, c0:c0 + 128].bitcast(FP8X4), lhsT_scale=zs[b][:, c0:c0 + 128],
@@ -221,17 +225,19 @@ def tile_cp_sparse_degree_lu_pb_t_kernel(tc, z, chain_lo, U_hi, masks_hi, C_w, C
             ch, h = divmod(b, 2)
             oh[b] = stream.tile([P, 1024], BF16, name="oh", tag="oh", bufs=LAG + 2)
             tmp = stream.tile([P, 512], F32, name="tmp", tag="tmp", bufs=2)
-            for s in range(2):
-                c0 = (2 * h + s) * K
-                nc.vector.scalar_tensor_tensor(out=oh[b][:, 512 * s:512 * s + 256], in0=y2[(b, s)][:, 0:256],
-                                               scalar=1.0, in1=cn[ch][:, c0 + 512:c0 + 768], op0=ADD, op1=MULT)
-                nc.vector.scalar_tensor_tensor(out=tmp[:, 256 * s:256 * s + 256], in0=y2[(b, s)][:, 256:512],
-                                               scalar=1.0, in1=cn[ch][:, c0 + 768:c0 + 1024], op0=ADD, op1=MULT)
-                if s == 0:
-                    between()
-            nc.vector.scalar_tensor_tensor(out=oh[b][:].rearrange("p (s r) -> p s r", s=2)[:, :, 256:512],
+            oh3 = oh[b][:].rearrange("p (s r) -> p s r", s=2)
+            tmp3 = tmp[:].rearrange("p (s r) -> p s r", s=2)
+            cn3 = cn[ch][:].rearrange("p (j c) -> p j c", j=4)
+            nc.vector.scalar_tensor_tensor(out=oh3[:, :, 0:256],
+                                           in0=y2[(b, 0)][:].rearrange("p (s r) -> p s r", s=2), scalar=1.0,
+                                           in1=cn3[:, 2 * h:2 * h + 2, 512:768], op0=ADD, op1=MULT)
+            nc.vector.scalar_tensor_tensor(out=tmp3,
+                                           in0=y2[(b, 1)][:].rearrange("p (s r) -> p s r", s=2), scalar=1.0,
+                                           in1=cn3[:, 2 * h:2 * h + 2, 768:1024], op0=ADD, op1=MULT)
+            between()
+            nc.vector.scalar_tensor_tensor(out=oh3[:, :, 256:512],
                                            in0=y3[b][:].rearrange("p (s r) -> p s r", s=2), scalar=1.0,
-                                           in1=tmp[:].rearrange("p (s r) -> p s r", s=2), op0=ADD, op1=MULT)
+                                           in1=tmp3, op0=ADD, op1=MULT)
 
         def t_o(b):
             ch, h = divmod(b, 2)
@@ -239,14 +245,14 @@ def tile_cp_sparse_degree_lu_pb_t_kernel(tc, z, chain_lo, U_hi, masks_hi, C_w, C
             og[b] = stream.tile([P, 2048], BF16, name="og", tag="og", bufs=2, align_bytes=64)
             ogw = og[b][:].bitcast(F32).rearrange("p (s g r u) -> p s g r u", s=2, g=2, u=2)
             ogb = og[b][:].rearrange("p (s g r t) -> p s g r t", s=2, g=2, t=4)
-            bank = pst.tile([P, 512], F32, name="tcl", tag="tcl", bufs=1)
+            bank = pst.tile([P, 512], F32, name="tcl", tag="t")
             for s in range(2):
                 j = 2 * h + s
                 for u in range(2):
                     nc.tensor.transpose(bank[:, 256 * s + 128 * u:256 * s + 128 * u + 128],
                                         cw_[:, 512 * j + 128 * u:512 * j + 128 * u + 128], ident_f[:])
             nc.scalar.copy(out=ogw[:, :, 0], in_=bank[:].rearrange("p (s u r) -> p s r u", s=2, u=2))
-            bankb = pst.tile([P, 1024], BF16, name="toh", tag="toh", bufs=1)
+            bankb = pst.tile([P, 1024], BF16, name="toh", tag="t")
             for s in range(2):
                 for t in range(4):
                     nc.tensor.transpose(bankb[:, 512 * s + 128 * t:512 * s + 128 * t + 128],
@@ -260,7 +266,7 @@ def tile_cp_sparse_degree_lu_pb_t_kernel(tc, z, chain_lo, U_hi, masks_hi, C_w, C
 
         def s_2(b):
             for s in range(2):
-                xp[(b, s)] = psm.tile([P, 512], F32, name="xp", tag="mx")
+                xp[(b, s)] = psm.tile([P, 512], F32, name="xp", tag="xp%d" % s)
                 for g in range(2):
                     c0 = (2 * s + g) * 128
                     nc.tensor.matmul_mx(out=xp[(b, s)][:],

@@ -16,12 +16,14 @@ TOKENS = 4096
 D = 1024
 K = 1024
 O = 512
-CHUNK = 512
-NCH = TOKENS // CHUNK
-NB = 2 * NCH
-LAG = 2
-ZBUFS = 5
-CBUFS = 5
+BATCH = 256
+NB = TOKENS // BATCH
+LAG_T = 2
+LAG_X = 2
+FILL = 1
+ZBUFS = 10
+CBUFS = 10
+OFFLOAD = False
 
 FLOPS = 2 * TOKENS * (512 * 1024 + 256 * 512 + 1024 * 512)
 BYTES = 3 * TOKENS * 1024 * 2 + 2 * (512 * 1024 + 256 * 512) * 2 + O * K * 2 + O * 2
@@ -35,9 +37,14 @@ def tile_cp_sparse_degree_lu_pb_t_kernel(tc, z, chain_lo, U_hi, masks_hi, C_w, C
     with ExitStack() as ctx:
         keep = ctx.enter_context(tc.tile_pool(name="keep", bufs=1))
         stream = ctx.enter_context(tc.tile_pool(name="stream", bufs=2))
-        pst = ctx.enter_context(tc.psum_pool(name="pst", bufs=3))
-        psm = ctx.enter_context(tc.psum_pool(name="psm", bufs=1))
+        psum = ctx.enter_context(tc.psum_pool(name="psum", bufs=8))
         ctx.enter_context(tc.manual_schedule())
+
+        def bank_f32():
+            return psum.tile([P, 512], F32, name="bank", tag="bank")
+
+        def bank_bf16():
+            return psum.tile([P, 1024], BF16, name="bankb", tag="bank")
 
         ident_f = keep.tile([P, P], F32, name="ident_f")
         ident_b = keep.tile([P, P], BF16, name="ident_b")
@@ -67,109 +74,119 @@ def tile_cp_sparse_degree_lu_pb_t_kernel(tc, z, chain_lo, U_hi, masks_hi, C_w, C
         zn = {}
         cn = {}
 
-        def rows(ap2d, ch):
-            return ap2d[ch * CHUNK:(ch + 1) * CHUNK, :].rearrange("(p j) c -> p j c", j=4)
+        def rows(ap2d, b):
+            return ap2d[b * BATCH:(b + 1) * BATCH, :].rearrange("(p s) c -> p s c", s=2)
 
-        def load_z(ch, halves=1):
-            zn[ch] = stream.tile([P, 4 * D], BF16, name="zn", tag="zn", bufs=ZBUFS)
-            dst = zn[ch][:].rearrange("p (j c) -> p j c", j=4)
-            src = rows(zf, ch)
-            step = 4 // halves
-            for h in range(halves):
-                nc.sync.dma_start(out=dst[:, h * step:(h + 1) * step, :], in_=src[:, h * step:(h + 1) * step, :])
+        def load_z(b):
+            zn[b] = stream.tile([P, 2 * D], BF16, name="zn", tag="zn", bufs=ZBUFS)
+            nc.sync.dma_start(out=zn[b][:].rearrange("p (s c) -> p s c", s=2), in_=rows(zf, b))
 
-        def load_c(ch):
-            cn[ch] = stream.tile([P, 4 * K], BF16, name="cn", tag="cn", bufs=CBUFS)
-            nc.sync.dma_start(out=cn[ch][:].rearrange("p (j c) -> p j c", j=4), in_=rows(chain_lo, ch))
+        def load_c(b, lo=0, hi=K):
+            if b not in cn:
+                cn[b] = stream.tile([P, 2 * K], BF16, name="cn", tag="cn", bufs=CBUFS)
+            nc.sync.dma_start(out=cn[b][:].rearrange("p (s c) -> p s c", s=2)[:, :, lo:hi],
+                              in_=rows(chain_lo, b)[:, :, lo:hi])
 
-        zn[0] = stream.tile([P, 4 * D], BF16, name="zn", tag="zn", bufs=ZBUFS)
-        z0dst = zn[0][:].rearrange("p (j c) -> p j c", j=4)
-        nc.sync.dma_start(out=z0dst[:, 0:2, :], in_=rows(zf, 0)[:, 0:2, :])
-        u_src = U_hi[0].rearrange("(t p) c -> p t c", p=P)
-        m_src = masks_hi[0].rearrange("(t p) c -> p t c", p=P)
-        u_dst = un[:].rearrange("p (t c) -> p t c", t=4)
-        m_dst = mn[:].rearrange("p (t c) -> p t c", t=4)
-        for h in range(2):
-            nc.sync.dma_start(out=u_dst[:, 2 * h:2 * h + 2, :], in_=u_src[:, 2 * h:2 * h + 2, :])
-            nc.sync.dma_start(out=m_dst[:, 2 * h:2 * h + 2, :], in_=m_src[:, 2 * h:2 * h + 2, :])
-        nc.sync.dma_start(out=z0dst[:, 2:4, :], in_=rows(zf, 0)[:, 2:4, :])
+        def load_w2(t):
+            nc.sync.dma_start(out=un[:, t * D:(t + 1) * D], in_=U_hi[0, t * P:(t + 1) * P, :])
+            nc.sync.dma_start(out=mn[:, t * D:(t + 1) * D], in_=masks_hi[0, t * P:(t + 1) * P, :])
+
+        load_w2(0)
+        load_w2(1)
+        load_z(0)
+        load_w2(2)
+        load_w2(3)
         nc.sync.dma_start(out=u3[:].rearrange("p (t c) -> p t c", t=2),
                           in_=U_hi[1, 256:512, 512:1024].rearrange("(t p) c -> p t c", p=P))
         nc.sync.dma_start(out=m3[:].rearrange("p (t c) -> p t c", t=2),
                           in_=masks_hi[1, 256:512, 512:1024].rearrange("(t p) c -> p t c", p=P))
-        load_c(0)
         load_z(1)
+        load_c(0, 512, K)
+        load_z(2)
+        load_c(0, 0, 512)
+        load_c(1)
+        load_z(3)
         nc.sync.dma_start(out=cwn[:].rearrange("p (t c) -> p t c", t=4),
                           in_=C_w.rearrange("(t p) c -> p t c", p=P))
         nc.sync.dma_start(out=brow[0:1, :], in_=C_b.unsqueeze(0))
-        load_c(1)
-        for ch in range(2, ZBUFS):
-            load_z(ch)
-            load_c(ch)
+        for b in range(2, CBUFS):
+            load_c(b)
+            if b + 2 < ZBUFS:
+                load_z(b + 2)
 
-        def prep_w23():
-            unw = un[:].bitcast(F32)
-            w2gw = w2g[:].bitcast(F32).rearrange("p (g r u) -> p g r u", g=2, u=2)
-            for h in range(2):
-                for tl in range(2):
-                    t = 2 * h + tl
-                    nc.vector.tensor_tensor(out=un[:, t * D:(t + 1) * D], in0=un[:, t * D:(t + 1) * D],
-                                            in1=mn[:, t * D:(t + 1) * D], op=MULT)
-                for g in range(2):
-                    bank = pst.tile([P, 512], F32, name="tw", tag="t")
-                    for u in range(2):
-                        for tl in range(2):
-                            t = 2 * h + tl
-                            w0 = t * 512 + 256 * g + 128 * u
-                            nc.tensor.transpose(bank[:, 256 * u + 128 * tl:256 * u + 128 * tl + 128],
-                                                unw[:, w0:w0 + 128], ident_f[:])
-                    nc.vector.tensor_copy(out=w2gw[:, g, 256 * h:256 * h + 256, :],
-                                          in_=bank[:].rearrange("p (u r) -> p r u", u=2))
-            nc.vector.tensor_tensor(out=u3[:], in0=u3[:], in1=m3[:], op=MULT)
+        unw = un[:].bitcast(F32)
+        w2gw = w2g[:].bitcast(F32).rearrange("p (g r u) -> p g r u", g=2, u=2)
+
+        def mask_w2(t):
+            nc.vector.tensor_tensor(out=un[:, t * D:(t + 1) * D], in0=un[:, t * D:(t + 1) * D],
+                                    in1=mn[:, t * D:(t + 1) * D], op=MULT)
+
+        def transpose_w2(t):
+            bank = bank_f32()
+            for gu in range(4):
+                nc.tensor.transpose(bank[:, 128 * gu:128 * gu + 128],
+                                    unw[:, 512 * t + 128 * gu:512 * t + 128 * gu + 128], ident_f[:])
+            nc.scalar.copy(out=w2gw[:, :, 128 * t:128 * t + 128, :],
+                           in_=bank[:].rearrange("p (g u r) -> p g r u", g=2, u=2))
+
+        def quantise_w2(half):
             for g in range(2):
-                nc.vector.quantize_mx(out=w2c[:, 512 * g:512 * g + 512].bitcast(FP8X4),
-                                      scales=w2s[:, 512 * g:512 * g + 512],
-                                      in_=w2g[:, 2048 * g:2048 * g + 2048])
+                c0 = 512 * g + 256 * half
+                nc.vector.quantize_mx(out=w2c[:, c0:c0 + 256].bitcast(FP8X4), scales=w2s[:, c0:c0 + 256],
+                                      in_=w2g[:, 4 * c0:4 * c0 + 1024])
+
+        def prep_w3():
+            nc.vector.tensor_tensor(out=u3[:], in0=u3[:], in1=m3[:], op=MULT)
             u3w = u3[:].bitcast(F32)
-            bank = pst.tile([P, 512], F32, name="tw", tag="t")
+            bank = bank_f32()
             for u in range(2):
                 for tl in range(2):
                     w0 = tl * 256 + 128 * u
                     nc.tensor.transpose(bank[:, 256 * u + 128 * tl:256 * u + 128 * tl + 128],
                                         u3w[:, w0:w0 + 128], ident_f[:])
-            nc.vector.tensor_copy(out=w3g[:].bitcast(F32).rearrange("p (r u) -> p r u", u=2),
-                                  in_=bank[:].rearrange("p (u r) -> p r u", u=2))
+            nc.scalar.copy(out=w3g[:].bitcast(F32).rearrange("p (r u) -> p r u", u=2),
+                           in_=bank[:].rearrange("p (u r) -> p r u", u=2))
+
+        def quantise_w3():
             nc.vector.quantize_mx(out=w3c[:].bitcast(FP8X4), scales=w3s[:], in_=w3g[:])
 
-        def prep_cw():
-            cww = cwn[:].bitcast(F32)
-            cwgw = cwg[:].bitcast(F32).rearrange("p (g r u) -> p g r u", g=2, u=2)
-            cwgb = cwg[:].rearrange("p (g r t) -> p g r t", g=2, t=4)
+        cww = cwn[:].bitcast(F32)
+        cwgw = cwg[:].bitcast(F32).rearrange("p (g r u) -> p g r u", g=2, u=2)
+        cwgb = cwg[:].rearrange("p (g r t) -> p g r t", g=2, t=4)
+
+        def quantise_cw(g):
+            nc.vector.quantize_mx(out=cwc[:, 512 * g:512 * g + 512].bitcast(FP8X4),
+                                  scales=cws[:, 512 * g:512 * g + 512], in_=cwg[:, 2048 * g:2048 * g + 2048])
+
+        def prep_cw_low():
             for h in range(2):
-                bank = pst.tile([P, 512], F32, name="tw", tag="t")
+                bank = bank_f32()
                 for u in range(2):
                     for tl in range(2):
                         w0 = (2 * h + tl) * 512 + 128 * u
                         nc.tensor.transpose(bank[:, 256 * u + 128 * tl:256 * u + 128 * tl + 128],
                                             cww[:, w0:w0 + 128], ident_f[:])
-                nc.vector.tensor_copy(out=cwgw[:, 0, 256 * h:256 * h + 256, :],
-                                      in_=bank[:].rearrange("p (u r) -> p r u", u=2))
-            for h in range(2):
-                bankb = pst.tile([P, 1024], BF16, name="twb", tag="t")
-                for t in range(4):
-                    for tl in range(2):
-                        c0 = (2 * h + tl) * K + 512 + 128 * t
-                        nc.tensor.transpose(bankb[:, 256 * t + 128 * tl:256 * t + 128 * tl + 128],
-                                            cwn[:, c0:c0 + 128], ident_b[:])
-                nc.vector.tensor_copy(out=cwgb[:, 1, 256 * h:256 * h + 256, :],
-                                      in_=bankb[:].rearrange("p (t r) -> p r t", t=4))
-            for g in range(2):
-                nc.vector.quantize_mx(out=cwc[:, 512 * g:512 * g + 512].bitcast(FP8X4),
-                                      scales=cws[:, 512 * g:512 * g + 512],
-                                      in_=cwg[:, 2048 * g:2048 * g + 2048])
-            bb = pst.tile([P, 512], F32, name="tbias", tag="t")
+                nc.scalar.copy(out=cwgw[:, 0, 256 * h:256 * h + 256, :],
+                               in_=bank[:].rearrange("p (u r) -> p r u", u=2))
+            quantise_cw(0)
+
+        def prep_cw_high(h, on_vector):
+            bankb = bank_bf16()
+            for t in range(4):
+                for tl in range(2):
+                    c0 = (2 * h + tl) * K + 512 + 128 * t
+                    nc.tensor.transpose(bankb[:, 256 * t + 128 * tl:256 * t + 128 * tl + 128],
+                                        cwn[:, c0:c0 + 128], ident_b[:])
+            src = bankb[:].rearrange("p (t r) -> p r t", t=4)
+            if on_vector:
+                nc.vector.tensor_copy(out=cwgb[:, 1, 256 * h:256 * h + 256, :], in_=src)
+            else:
+                nc.scalar.copy(out=cwgb[:, 1, 256 * h:256 * h + 256, :], in_=src)
+
+        def prep_bias():
+            bb = bank_f32()
             nc.tensor.matmul(out=bb[:], lhsT=ones[:], rhs=brow[:], start=True, stop=True)
-            nc.vector.tensor_copy(out=bias[:], in_=bb[:])
+            nc.scalar.copy(out=bias[:], in_=bb[:])
 
         zg = {}
         zc = {}
@@ -179,20 +196,18 @@ def tile_cp_sparse_degree_lu_pb_t_kernel(tc, z, chain_lo, U_hi, masks_hi, C_w, C
         oh = {}
         og = {}
         oc = {}
-        os_ = {}
+        osc = {}
         xp = {}
 
         def t_z(b):
-            ch, h = divmod(b, 2)
-            zw = zn[ch][:].bitcast(F32)
+            zw = zn[b][:].bitcast(F32)
             zg[b] = stream.tile([P, 2048], BF16, name="zg", tag="zg", bufs=2, align_bytes=64)
             zgw = zg[b][:].bitcast(F32).rearrange("p (s g r u) -> p s g r u", s=2, g=2, u=2)
             for s in range(2):
-                j = 2 * h + s
-                bank = pst.tile([P, 512], F32, name="tz", tag="t")
+                bank = bank_f32()
                 for gu in range(4):
                     nc.tensor.transpose(bank[:, 128 * gu:128 * gu + 128],
-                                        zw[:, 512 * j + 128 * gu:512 * j + 128 * gu + 128], ident_f[:])
+                                        zw[:, 512 * s + 128 * gu:512 * s + 128 * gu + 128], ident_f[:])
                 nc.scalar.copy(out=zgw[:, s], in_=bank[:].rearrange("p (g u r) -> p g r u", g=2, u=2))
 
         def q_z(b):
@@ -201,10 +216,8 @@ def tile_cp_sparse_degree_lu_pb_t_kernel(tc, z, chain_lo, U_hi, masks_hi, C_w, C
             nc.vector.quantize_mx(out=zc[b][:].bitcast(FP8X4), scales=zs[b][:], in_=zg[b][:])
 
         def s_1(b):
-            y2[(b, 0)] = psm.tile([P, 512], F32, name="y2a", tag="y2a")
-            y2[(b, 1)] = psm.tile([P, 512], F32, name="y2b", tag="y2b")
-            y3[b] = psm.tile([P, 512], F32, name="y3", tag="y3")
             for half in range(2):
+                y2[(b, half)] = bank_f32()
                 for s in range(2):
                     for g in range(2):
                         c0 = (2 * s + g) * 128
@@ -214,6 +227,7 @@ def tile_cp_sparse_degree_lu_pb_t_kernel(tc, z, chain_lo, U_hi, masks_hi, C_w, C
                                             lhsT_scale=zs[b][:, c0:c0 + 128],
                                             rhs=w2c[:, r0:r0 + 256].bitcast(FP8X4), rhs_scale=w2s[:, r0:r0 + 256],
                                             start=(g == 0), stop=(g == 1))
+            y3[b] = bank_f32()
             for s in range(2):
                 c0 = (2 * s + 1) * 128
                 nc.tensor.matmul_mx(out=y3[b][:, 256 * s:256 * s + 256],
@@ -221,38 +235,36 @@ def tile_cp_sparse_degree_lu_pb_t_kernel(tc, z, chain_lo, U_hi, masks_hi, C_w, C
                                     rhs=w3c[:].bitcast(FP8X4), rhs_scale=w3s[:],
                                     start=True, stop=True)
 
-        def chain(b, between):
-            ch, h = divmod(b, 2)
-            oh[b] = stream.tile([P, 1024], BF16, name="oh", tag="oh", bufs=LAG + 2)
+        def chain(b):
+            oh[b] = stream.tile([P, 1024], BF16, name="oh", tag="oh", bufs=LAG_T + 2)
             tmp = stream.tile([P, 512], F32, name="tmp", tag="tmp", bufs=2)
             oh3 = oh[b][:].rearrange("p (s r) -> p s r", s=2)
             tmp3 = tmp[:].rearrange("p (s r) -> p s r", s=2)
-            cn3 = cn[ch][:].rearrange("p (j c) -> p j c", j=4)
+            cn3 = cn[b][:].rearrange("p (s c) -> p s c", s=2)
             nc.vector.scalar_tensor_tensor(out=oh3[:, :, 0:256],
                                            in0=y2[(b, 0)][:].rearrange("p (s r) -> p s r", s=2), scalar=1.0,
-                                           in1=cn3[:, 2 * h:2 * h + 2, 512:768], op0=ADD, op1=MULT)
+                                           in1=cn3[:, :, 512:768], op0=ADD, op1=MULT)
             nc.vector.scalar_tensor_tensor(out=tmp3,
                                            in0=y2[(b, 1)][:].rearrange("p (s r) -> p s r", s=2), scalar=1.0,
-                                           in1=cn3[:, 2 * h:2 * h + 2, 768:1024], op0=ADD, op1=MULT)
-            between()
+                                           in1=cn3[:, :, 768:1024], op0=ADD, op1=MULT)
             nc.vector.scalar_tensor_tensor(out=oh3[:, :, 256:512],
                                            in0=y3[b][:].rearrange("p (s r) -> p s r", s=2), scalar=1.0,
                                            in1=tmp3, op0=ADD, op1=MULT)
 
-        def t_o(b):
-            ch, h = divmod(b, 2)
-            cw_ = cn[ch][:].bitcast(F32)
+        def t_c(b):
+            cw_ = cn[b][:].bitcast(F32)
             og[b] = stream.tile([P, 2048], BF16, name="og", tag="og", bufs=2, align_bytes=64)
             ogw = og[b][:].bitcast(F32).rearrange("p (s g r u) -> p s g r u", s=2, g=2, u=2)
-            ogb = og[b][:].rearrange("p (s g r t) -> p s g r t", s=2, g=2, t=4)
-            bank = pst.tile([P, 512], F32, name="tcl", tag="t")
+            bank = bank_f32()
             for s in range(2):
-                j = 2 * h + s
                 for u in range(2):
                     nc.tensor.transpose(bank[:, 256 * s + 128 * u:256 * s + 128 * u + 128],
-                                        cw_[:, 512 * j + 128 * u:512 * j + 128 * u + 128], ident_f[:])
+                                        cw_[:, 512 * s + 128 * u:512 * s + 128 * u + 128], ident_f[:])
             nc.scalar.copy(out=ogw[:, :, 0], in_=bank[:].rearrange("p (s u r) -> p s r u", s=2, u=2))
-            bankb = pst.tile([P, 1024], BF16, name="toh", tag="t")
+
+        def t_oh(b):
+            ogb = og[b][:].rearrange("p (s g r t) -> p s g r t", s=2, g=2, t=4)
+            bankb = bank_bf16()
             for s in range(2):
                 for t in range(4):
                     nc.tensor.transpose(bankb[:, 512 * s + 128 * t:512 * s + 128 * t + 128],
@@ -260,48 +272,89 @@ def tile_cp_sparse_degree_lu_pb_t_kernel(tc, z, chain_lo, U_hi, masks_hi, C_w, C
             nc.scalar.copy(out=ogb[:, :, 1], in_=bankb[:].rearrange("p (s t r) -> p s r t", s=2, t=4))
 
         def q_o(b):
-            oc[b] = stream.tile([P, 512], U32, name="oc", tag="oc", bufs=2, align_bytes=64)
-            os_[b] = stream.tile([P, 512], U8, name="os", tag="os", bufs=2, align_bytes=64)
-            nc.vector.quantize_mx(out=oc[b][:].bitcast(FP8X4), scales=os_[b][:], in_=og[b][:])
+            oc[b] = stream.tile([P, 512], U32, name="oc", tag="oc", bufs=LAG_X + 2, align_bytes=64)
+            osc[b] = stream.tile([P, 512], U8, name="osc", tag="osc", bufs=LAG_X + 2, align_bytes=64)
+            nc.vector.quantize_mx(out=oc[b][:].bitcast(FP8X4), scales=osc[b][:], in_=og[b][:])
 
         def s_2(b):
             for s in range(2):
-                xp[(b, s)] = psm.tile([P, 512], F32, name="xp", tag="xp%d" % s)
+                xp[(b, s)] = bank_f32()
                 for g in range(2):
                     c0 = (2 * s + g) * 128
                     nc.tensor.matmul_mx(out=xp[(b, s)][:],
-                                        lhsT=oc[b][:, c0:c0 + 128].bitcast(FP8X4), lhsT_scale=os_[b][:, c0:c0 + 128],
+                                        lhsT=oc[b][:, c0:c0 + 128].bitcast(FP8X4), lhsT_scale=osc[b][:, c0:c0 + 128],
                                         rhs=cwc[:, 512 * g:512 * g + 512].bitcast(FP8X4),
                                         rhs_scale=cws[:, 512 * g:512 * g + 512],
                                         start=(g == 0), stop=(g == 1))
 
         def e_x(b):
-            ch, h = divmod(b, 2)
-            xs = stream.tile([P, 1024], F32, name="xs", tag="xs", bufs=3)
-            for s in range(2):
-                nc.vector.tensor_tensor(out=xs[:, 512 * s:512 * s + 512], in0=xp[(b, s)][:], in1=bias[:], op=ADD)
-            nc.sync.dma_start(out=rows(xf, ch)[:, 2 * h:2 * h + 2, :], in_=xs[:].rearrange("p (s o) -> p s o", s=2))
+            xs = stream.tile([P, 1024], F32, name="xs", tag="xs", bufs=6)
+            if OFFLOAD:
+                nc.scalar.copy(out=xs[:, 0:512], in_=xp[(b, 0)][:])
+                nc.gpsimd.tensor_tensor(out=xs[:, 0:512], in0=xs[:, 0:512], in1=bias[:], op=ADD)
+            else:
+                nc.vector.tensor_tensor(out=xs[:, 0:512], in0=xp[(b, 0)][:], in1=bias[:], op=ADD)
+            nc.vector.tensor_tensor(out=xs[:, 512:1024], in0=xp[(b, 1)][:], in1=bias[:], op=ADD)
+            nc.sync.dma_start(out=rows(xf, b), in_=xs[:].rearrange("p (s o) -> p s o", s=2))
 
-        for k in range(NB + LAG + 1):
+        mask_w2(0)
+        transpose_w2(0)
+        mask_w2(1)
+        transpose_w2(1)
+        t_z(0)
+        mask_w2(2)
+        quantise_w2(0)
+        transpose_w2(2)
+        mask_w2(3)
+        transpose_w2(3)
+        q_z(0)
+        prep_w3()
+        quantise_w2(1)
+        quantise_w3()
+        load_z(ZBUFS)
+
+        for k in range(1, NB + 1):
+            b2 = k - LAG_T - 1 - LAG_X
             if k < NB:
                 t_z(k)
-            if k == 0:
-                q_z(0)
-                prep_w23()
-            if 0 <= k - LAG < NB:
-                t_o(k - LAG)
-            if 0 <= k - 1 < NB:
-                s_1(k - 1)
-                chain(k - 1, (lambda: q_z(k)) if k < NB else (lambda: None))
-            if 0 <= k - LAG - 1 < NB:
-                s_2(k - LAG - 1)
+            if k - LAG_T >= 0:
+                t_c(k - LAG_T)
+                t_oh(k - LAG_T)
+            if k == NB:
+                t_c(NB - 1)
+            s_1(k - 1)
+            chain(k - 1)
+            if k < NB:
+                q_z(k)
+            if b2 >= 0:
+                s_2(b2)
+            if k - LAG_T >= 0:
+                q_o(k - LAG_T)
+            if b2 >= 0:
+                e_x(b2)
             if k == 2:
-                prep_cw()
-            if 0 <= k - LAG < NB:
-                q_o(k - LAG)
-            if 0 <= k - LAG - 1 < NB:
-                e_x(k - LAG - 1)
-            if k % 2 == 1 and (k - 1) // 2 + ZBUFS < NCH:
-                load_z((k - 1) // 2 + ZBUFS)
-            if (k - 1 - LAG) >= 0 and (k - 1 - LAG) % 2 == 0 and (k - 1 - LAG) // 2 + CBUFS < NCH:
-                load_c((k - 1 - LAG) // 2 + CBUFS)
+                prep_cw_low()
+            if k == 3:
+                prep_cw_high(0, False)
+                prep_bias()
+            if k == 4:
+                prep_cw_high(1, True)
+                quantise_cw(1)
+            if k + ZBUFS < NB:
+                load_z(k + ZBUFS)
+            if k - LAG_T >= 0 and k - LAG_T + CBUFS < NB:
+                load_c(k - LAG_T + CBUFS)
+
+        first = NB - LAG_T - LAG_X
+        for b in range(first, first + FILL):
+            s_2(b)
+        t_oh(NB - 1)
+        for b in range(first, first + FILL):
+            e_x(b)
+        for b in range(first + FILL, NB - 1):
+            s_2(b)
+        q_o(NB - 1)
+        for b in range(first + FILL, NB - 1):
+            e_x(b)
+        s_2(NB - 1)
+        e_x(NB - 1)

@@ -23,7 +23,6 @@ LAG_X = 2
 FILL = 1
 ZBUFS = 10
 CBUFS = 10
-OFFLOAD = False
 
 FLOPS = 2 * TOKENS * (512 * 1024 + 256 * 512 + 1024 * 512)
 BYTES = 3 * TOKENS * 1024 * 2 + 2 * (512 * 1024 + 256 * 512) * 2 + O * K * 2 + O * 2
@@ -287,15 +286,25 @@ def tile_cp_sparse_degree_lu_pb_t_kernel(tc, z, chain_lo, U_hi, masks_hi, C_w, C
                                         rhs_scale=cws[:, 512 * g:512 * g + 512],
                                         start=(g == 0), stop=(g == 1))
 
+        xs = {}
+
+        def e_x_vector(b, s):
+            if b not in xs:
+                xs[b] = stream.tile([P, 1024], F32, name="xs", tag="xs", bufs=6)
+            nc.vector.tensor_tensor(out=xs[b][:, 512 * s:512 * s + 512], in0=xp[(b, s)][:], in1=bias[:], op=ADD)
+
+        def e_x_scalar(b, s):
+            nc.scalar.copy(out=xs[b][:, 512 * s:512 * s + 512], in_=xp[(b, s)][:])
+            nc.gpsimd.tensor_tensor(out=xs[b][:, 512 * s:512 * s + 512], in0=xs[b][:, 512 * s:512 * s + 512],
+                                    in1=bias[:], op=ADD)
+
+        def store(b):
+            nc.sync.dma_start(out=rows(xf, b), in_=xs[b][:].rearrange("p (s o) -> p s o", s=2))
+
         def e_x(b):
-            xs = stream.tile([P, 1024], F32, name="xs", tag="xs", bufs=6)
-            if OFFLOAD:
-                nc.scalar.copy(out=xs[:, 0:512], in_=xp[(b, 0)][:])
-                nc.gpsimd.tensor_tensor(out=xs[:, 0:512], in0=xs[:, 0:512], in1=bias[:], op=ADD)
-            else:
-                nc.vector.tensor_tensor(out=xs[:, 0:512], in0=xp[(b, 0)][:], in1=bias[:], op=ADD)
-            nc.vector.tensor_tensor(out=xs[:, 512:1024], in0=xp[(b, 1)][:], in1=bias[:], op=ADD)
-            nc.sync.dma_start(out=rows(xf, b), in_=xs[:].rearrange("p (s o) -> p s o", s=2))
+            e_x_vector(b, 0)
+            e_x_vector(b, 1)
+            store(b)
 
         mask_w2(0)
         transpose_w2(0)
@@ -313,10 +322,15 @@ def tile_cp_sparse_degree_lu_pb_t_kernel(tc, z, chain_lo, U_hi, masks_hi, C_w, C
         quantise_w3()
         load_z(ZBUFS)
 
+        pending = -1
         for k in range(1, NB + 1):
             b2 = k - LAG_T - 1 - LAG_X
             if k < NB:
                 t_z(k)
+            if pending >= 0:
+                e_x_scalar(pending, 0)
+                store(pending)
+                pending = -1
             if k - LAG_T >= 0:
                 t_c(k - LAG_T)
                 t_oh(k - LAG_T)
@@ -328,10 +342,10 @@ def tile_cp_sparse_degree_lu_pb_t_kernel(tc, z, chain_lo, U_hi, masks_hi, C_w, C
                 q_z(k)
             if b2 >= 0:
                 s_2(b2)
+                e_x_vector(b2, 1)
+                pending = b2
             if k - LAG_T >= 0:
                 q_o(k - LAG_T)
-            if b2 >= 0:
-                e_x(b2)
             if k == 2:
                 prep_cw_low()
             if k == 3:
@@ -348,6 +362,8 @@ def tile_cp_sparse_degree_lu_pb_t_kernel(tc, z, chain_lo, U_hi, masks_hi, C_w, C
         first = NB - LAG_T - LAG_X
         for b in range(first, first + FILL):
             s_2(b)
+        e_x_scalar(pending, 0)
+        store(pending)
         t_oh(NB - 1)
         for b in range(first, first + FILL):
             e_x(b)

@@ -18,9 +18,7 @@ K = 1024
 O = 512
 BATCH = 256
 NB = TOKENS // BATCH
-LAG_T = 2
-LAG_X = 2
-FILL = 1
+LAG_X = 1
 ZBUFS = 10
 CBUFS = 10
 
@@ -42,13 +40,8 @@ def tile_cp_sparse_degree_lu_pb_t_kernel(tc, z, chain_lo, U_hi, masks_hi, C_w, C
         def bank_f32():
             return psum.tile([P, 512], F32, name="bank", tag="bank")
 
-        def bank_bf16():
-            return psum.tile([P, 1024], BF16, name="bankb", tag="bank")
-
         ident_f = keep.tile([P, P], F32, name="ident_f")
-        ident_b = keep.tile([P, P], BF16, name="ident_b")
         make_identity(nc, ident_f[:])
-        make_identity(nc, ident_b[:])
         ones = keep.tile([P, P], BF16, name="ones")
         brow = keep.tile([P, O], BF16, name="brow")
         bias = keep.tile([P, O], F32, name="bias")
@@ -80,38 +73,36 @@ def tile_cp_sparse_degree_lu_pb_t_kernel(tc, z, chain_lo, U_hi, masks_hi, C_w, C
             zn[b] = stream.tile([P, 2 * D], BF16, name="zn", tag="zn", bufs=ZBUFS)
             nc.sync.dma_start(out=zn[b][:].rearrange("p (s c) -> p s c", s=2), in_=rows(zf, b))
 
-        def load_c(b, lo=0, hi=K):
-            if b not in cn:
-                cn[b] = stream.tile([P, 2 * K], BF16, name="cn", tag="cn", bufs=CBUFS)
-            nc.sync.dma_start(out=cn[b][:].rearrange("p (s c) -> p s c", s=2)[:, :, lo:hi],
-                              in_=rows(chain_lo, b)[:, :, lo:hi])
+        def load_c(b):
+            cn[b] = stream.tile([P, 2 * K], BF16, name="cn", tag="cn", bufs=CBUFS)
+            nc.sync.dma_start(out=cn[b][:].rearrange("p (s c) -> p s c", s=2), in_=rows(chain_lo, b))
 
         def load_w2(t):
-            nc.sync.dma_start(out=un[:, t * D:(t + 1) * D], in_=U_hi[0, t * P:(t + 1) * P, :])
-            nc.sync.dma_start(out=mn[:, t * D:(t + 1) * D], in_=masks_hi[0, t * P:(t + 1) * P, :])
+            kind, par = divmod(t, 2)
+            for dst, src in ((un, U_hi), (mn, masks_hi)):
+                nc.sync.dma_start(out=dst[:, t * D:(t + 1) * D],
+                                  in_=src[0, 256 * kind:256 * kind + 256, :].rearrange("(m e) c -> m e c", e=2)[:, par, :])
 
         load_w2(0)
         load_w2(1)
         load_z(0)
         load_w2(2)
         load_w2(3)
-        nc.sync.dma_start(out=u3[:].rearrange("p (t c) -> p t c", t=2),
-                          in_=U_hi[1, 256:512, 512:1024].rearrange("(t p) c -> p t c", p=P))
-        nc.sync.dma_start(out=m3[:].rearrange("p (t c) -> p t c", t=2),
-                          in_=masks_hi[1, 256:512, 512:1024].rearrange("(t p) c -> p t c", p=P))
+        nc.sync.dma_start(out=u3[:].rearrange("p (e c) -> p e c", e=2),
+                          in_=U_hi[1, 256:512, 512:1024].rearrange("(m e) c -> m e c", e=2))
+        nc.sync.dma_start(out=m3[:].rearrange("p (e c) -> p e c", e=2),
+                          in_=masks_hi[1, 256:512, 512:1024].rearrange("(m e) c -> m e c", e=2))
+        load_c(0)
         load_z(1)
-        load_c(0, 512, K)
-        load_z(2)
-        load_c(0, 0, 512)
         load_c(1)
-        load_z(3)
+        load_z(2)
         nc.sync.dma_start(out=cwn[:].rearrange("p (t c) -> p t c", t=4),
                           in_=C_w.rearrange("(t p) c -> p t c", p=P))
         nc.sync.dma_start(out=brow[0:1, :], in_=C_b.unsqueeze(0))
         for b in range(2, CBUFS):
             load_c(b)
-            if b + 2 < ZBUFS:
-                load_z(b + 2)
+            if b + 1 < ZBUFS:
+                load_z(b + 1)
 
         unw = un[:].bitcast(F32)
         w2gw = w2g[:].bitcast(F32).rearrange("p (g r u) -> p g r u", g=2, u=2)
@@ -151,36 +142,22 @@ def tile_cp_sparse_degree_lu_pb_t_kernel(tc, z, chain_lo, U_hi, masks_hi, C_w, C
 
         cww = cwn[:].bitcast(F32)
         cwgw = cwg[:].bitcast(F32).rearrange("p (g r u) -> p g r u", g=2, u=2)
-        cwgb = cwg[:].rearrange("p (g r t) -> p g r t", g=2, t=4)
 
         def quantise_cw(g):
             nc.vector.quantize_mx(out=cwc[:, 512 * g:512 * g + 512].bitcast(FP8X4),
                                   scales=cws[:, 512 * g:512 * g + 512], in_=cwg[:, 2048 * g:2048 * g + 2048])
 
-        def prep_cw_low():
+        def prep_cw(g):
             for h in range(2):
                 bank = bank_f32()
                 for u in range(2):
                     for tl in range(2):
-                        w0 = (2 * h + tl) * 512 + 128 * u
+                        w0 = (2 * h + tl) * 512 + 256 * g + 128 * u
                         nc.tensor.transpose(bank[:, 256 * u + 128 * tl:256 * u + 128 * tl + 128],
                                             cww[:, w0:w0 + 128], ident_f[:])
-                nc.scalar.copy(out=cwgw[:, 0, 256 * h:256 * h + 256, :],
+                nc.scalar.copy(out=cwgw[:, g, 256 * h:256 * h + 256, :],
                                in_=bank[:].rearrange("p (u r) -> p r u", u=2))
-            quantise_cw(0)
-
-        def prep_cw_high(h, on_vector):
-            bankb = bank_bf16()
-            for t in range(4):
-                for tl in range(2):
-                    c0 = (2 * h + tl) * K + 512 + 128 * t
-                    nc.tensor.transpose(bankb[:, 256 * t + 128 * tl:256 * t + 128 * tl + 128],
-                                        cwn[:, c0:c0 + 128], ident_b[:])
-            src = bankb[:].rearrange("p (t r) -> p r t", t=4)
-            if on_vector:
-                nc.vector.tensor_copy(out=cwgb[:, 1, 256 * h:256 * h + 256, :], in_=src)
-            else:
-                nc.scalar.copy(out=cwgb[:, 1, 256 * h:256 * h + 256, :], in_=src)
+            quantise_cw(g)
 
         def prep_bias():
             bb = bank_f32()
@@ -192,7 +169,6 @@ def tile_cp_sparse_degree_lu_pb_t_kernel(tc, z, chain_lo, U_hi, masks_hi, C_w, C
         zs = {}
         y2 = {}
         y3 = {}
-        oh = {}
         og = {}
         oc = {}
         osc = {}
@@ -201,74 +177,64 @@ def tile_cp_sparse_degree_lu_pb_t_kernel(tc, z, chain_lo, U_hi, masks_hi, C_w, C
         def t_z(b):
             zw = zn[b][:].bitcast(F32)
             zg[b] = stream.tile([P, 2048], BF16, name="zg", tag="zg", bufs=2, align_bytes=64)
-            zgw = zg[b][:].bitcast(F32).rearrange("p (s g r u) -> p s g r u", s=2, g=2, u=2)
+            zgw = zg[b][:].bitcast(F32).rearrange("p (g s r u) -> p g s r u", g=2, s=2, u=2)
             for s in range(2):
                 bank = bank_f32()
                 for gu in range(4):
                     nc.tensor.transpose(bank[:, 128 * gu:128 * gu + 128],
                                         zw[:, 512 * s + 128 * gu:512 * s + 128 * gu + 128], ident_f[:])
-                nc.scalar.copy(out=zgw[:, s], in_=bank[:].rearrange("p (g u r) -> p g r u", g=2, u=2))
+                nc.scalar.copy(out=zgw[:, :, s], in_=bank[:].rearrange("p (g u r) -> p g r u", g=2, u=2))
 
         def q_z(b):
             zc[b] = stream.tile([P, 512], U32, name="zc", tag="zc", bufs=2, align_bytes=64)
             zs[b] = stream.tile([P, 512], U8, name="zs", tag="zs", bufs=2, align_bytes=64)
             nc.vector.quantize_mx(out=zc[b][:].bitcast(FP8X4), scales=zs[b][:], in_=zg[b][:])
 
+        def t_c(b):
+            cw_ = cn[b][:].bitcast(F32)
+            og[b] = stream.tile([P, 2048], BF16, name="og", tag="og", bufs=3, align_bytes=64)
+            ogw = og[b][:].bitcast(F32).rearrange("p (g t u) -> p g t u", g=2, u=2)
+            for g in range(2):
+                bank = bank_f32()
+                for u in range(2):
+                    for s in range(2):
+                        w0 = 512 * s + 256 * g + 128 * u
+                        nc.tensor.transpose(bank[:, 256 * u + 128 * s:256 * u + 128 * s + 128],
+                                            cw_[:, w0:w0 + 128], ident_f[:])
+                nc.scalar.copy(out=ogw[:, g], in_=bank[:].rearrange("p (u t) -> p t u", u=2))
+
         def s_1(b):
-            for half in range(2):
-                y2[(b, half)] = bank_f32()
-                for s in range(2):
+            for kind in range(2):
+                y2[(b, kind)] = bank_f32()
+                for e in range(2):
                     for g in range(2):
-                        c0 = (2 * s + g) * 128
-                        r0 = 512 * g + 256 * half
-                        nc.tensor.matmul_mx(out=y2[(b, half)][:, 256 * s:256 * s + 256],
-                                            lhsT=zc[b][:, c0:c0 + 128].bitcast(FP8X4),
-                                            lhsT_scale=zs[b][:, c0:c0 + 128],
-                                            rhs=w2c[:, r0:r0 + 256].bitcast(FP8X4), rhs_scale=w2s[:, r0:r0 + 256],
+                        w0 = 512 * g + 128 * (2 * kind + e)
+                        nc.tensor.matmul_mx(out=y2[(b, kind)][:, 256 * e:256 * e + 256],
+                                            lhsT=w2c[:, w0:w0 + 128].bitcast(FP8X4), lhsT_scale=w2s[:, w0:w0 + 128],
+                                            rhs=zc[b][:, 256 * g:256 * g + 256].bitcast(FP8X4),
+                                            rhs_scale=zs[b][:, 256 * g:256 * g + 256],
                                             start=(g == 0), stop=(g == 1))
             y3[b] = bank_f32()
-            for s in range(2):
-                c0 = (2 * s + 1) * 128
-                nc.tensor.matmul_mx(out=y3[b][:, 256 * s:256 * s + 256],
-                                    lhsT=zc[b][:, c0:c0 + 128].bitcast(FP8X4), lhsT_scale=zs[b][:, c0:c0 + 128],
-                                    rhs=w3c[:].bitcast(FP8X4), rhs_scale=w3s[:],
+            for e in range(2):
+                nc.tensor.matmul_mx(out=y3[b][:, 256 * e:256 * e + 256],
+                                    lhsT=w3c[:, 128 * e:128 * e + 128].bitcast(FP8X4),
+                                    lhsT_scale=w3s[:, 128 * e:128 * e + 128],
+                                    rhs=zc[b][:, 256:512].bitcast(FP8X4), rhs_scale=zs[b][:, 256:512],
                                     start=True, stop=True)
 
         def chain(b):
-            oh[b] = stream.tile([P, 1024], BF16, name="oh", tag="oh", bufs=LAG_T + 2)
             tmp = stream.tile([P, 512], F32, name="tmp", tag="tmp", bufs=2)
-            oh3 = oh[b][:].rearrange("p (s r) -> p s r", s=2)
-            tmp3 = tmp[:].rearrange("p (s r) -> p s r", s=2)
-            cn3 = cn[b][:].rearrange("p (s c) -> p s c", s=2)
-            nc.vector.scalar_tensor_tensor(out=oh3[:, :, 0:256],
-                                           in0=y2[(b, 0)][:].rearrange("p (s r) -> p s r", s=2), scalar=1.0,
-                                           in1=cn3[:, :, 512:768], op0=ADD, op1=MULT)
+            tmp3 = tmp[:].rearrange("p (t e) -> p t e", e=2)
+            hi = og[b][:].rearrange("p (g t v) -> p g t v", g=2, v=4)
+            nc.vector.scalar_tensor_tensor(out=hi[:, 1, :, 0:2],
+                                           in0=y2[(b, 0)][:].rearrange("p (e t) -> p t e", e=2), scalar=1.0,
+                                           in1=hi[:, 1, :, 0:2], op0=ADD, op1=MULT)
             nc.vector.scalar_tensor_tensor(out=tmp3,
-                                           in0=y2[(b, 1)][:].rearrange("p (s r) -> p s r", s=2), scalar=1.0,
-                                           in1=cn3[:, :, 768:1024], op0=ADD, op1=MULT)
-            nc.vector.scalar_tensor_tensor(out=oh3[:, :, 256:512],
-                                           in0=y3[b][:].rearrange("p (s r) -> p s r", s=2), scalar=1.0,
+                                           in0=y2[(b, 1)][:].rearrange("p (e t) -> p t e", e=2), scalar=1.0,
+                                           in1=hi[:, 1, :, 2:4], op0=ADD, op1=MULT)
+            nc.vector.scalar_tensor_tensor(out=hi[:, 1, :, 2:4],
+                                           in0=y3[b][:].rearrange("p (e t) -> p t e", e=2), scalar=1.0,
                                            in1=tmp3, op0=ADD, op1=MULT)
-
-        def t_c(b):
-            cw_ = cn[b][:].bitcast(F32)
-            og[b] = stream.tile([P, 2048], BF16, name="og", tag="og", bufs=2, align_bytes=64)
-            ogw = og[b][:].bitcast(F32).rearrange("p (s g r u) -> p s g r u", s=2, g=2, u=2)
-            bank = bank_f32()
-            for s in range(2):
-                for u in range(2):
-                    nc.tensor.transpose(bank[:, 256 * s + 128 * u:256 * s + 128 * u + 128],
-                                        cw_[:, 512 * s + 128 * u:512 * s + 128 * u + 128], ident_f[:])
-            nc.scalar.copy(out=ogw[:, :, 0], in_=bank[:].rearrange("p (s u r) -> p s r u", s=2, u=2))
-
-        def t_oh(b):
-            ogb = og[b][:].rearrange("p (s g r t) -> p s g r t", s=2, g=2, t=4)
-            bankb = bank_bf16()
-            for s in range(2):
-                for t in range(4):
-                    nc.tensor.transpose(bankb[:, 512 * s + 128 * t:512 * s + 128 * t + 128],
-                                        oh[b][:, 512 * s + 128 * t:512 * s + 128 * t + 128], ident_b[:])
-            nc.scalar.copy(out=ogb[:, :, 1], in_=bankb[:].rearrange("p (s t r) -> p s r t", s=2, t=4))
 
         def q_o(b):
             oc[b] = stream.tile([P, 512], U32, name="oc", tag="oc", bufs=LAG_X + 2, align_bytes=64)
@@ -279,7 +245,7 @@ def tile_cp_sparse_degree_lu_pb_t_kernel(tc, z, chain_lo, U_hi, masks_hi, C_w, C
             for s in range(2):
                 xp[(b, s)] = bank_f32()
                 for g in range(2):
-                    c0 = (2 * s + g) * 128
+                    c0 = 256 * g + 128 * s
                     nc.tensor.matmul_mx(out=xp[(b, s)][:],
                                         lhsT=oc[b][:, c0:c0 + 128].bitcast(FP8X4), lhsT_scale=osc[b][:, c0:c0 + 128],
                                         rhs=cwc[:, 512 * g:512 * g + 512].bitcast(FP8X4),
@@ -294,6 +260,8 @@ def tile_cp_sparse_degree_lu_pb_t_kernel(tc, z, chain_lo, U_hi, masks_hi, C_w, C
             nc.vector.tensor_tensor(out=xs[b][:, 512 * s:512 * s + 512], in0=xp[(b, s)][:], in1=bias[:], op=ADD)
 
         def e_x_scalar(b, s):
+            if b not in xs:
+                xs[b] = stream.tile([P, 1024], F32, name="xs", tag="xs", bufs=6)
             nc.scalar.copy(out=xs[b][:, 512 * s:512 * s + 512], in_=xp[(b, s)][:])
             nc.gpsimd.tensor_tensor(out=xs[b][:, 512 * s:512 * s + 512], in0=xs[b][:, 512 * s:512 * s + 512],
                                     in1=bias[:], op=ADD)
@@ -320,57 +288,43 @@ def tile_cp_sparse_degree_lu_pb_t_kernel(tc, z, chain_lo, U_hi, masks_hi, C_w, C
         prep_w3()
         quantise_w2(1)
         quantise_w3()
+        t_c(0)
         load_z(ZBUFS)
 
         pending = -1
         for k in range(1, NB + 1):
-            b2 = k - LAG_T - 1 - LAG_X
+            b2 = k - 2 - LAG_X
             if k < NB:
                 t_z(k)
             if pending >= 0:
                 e_x_scalar(pending, 0)
+                e_x_scalar(pending, 1)
                 store(pending)
                 pending = -1
-            if k - LAG_T >= 0:
-                t_c(k - LAG_T)
-                t_oh(k - LAG_T)
-            if k == NB:
-                t_c(NB - 1)
+            if k < NB:
+                t_c(k)
             s_1(k - 1)
-            chain(k - 1)
             if k < NB:
                 q_z(k)
+            chain(k - 1)
             if b2 >= 0:
                 s_2(b2)
-                e_x_vector(b2, 1)
                 pending = b2
-            if k - LAG_T >= 0:
-                q_o(k - LAG_T)
+            q_o(k - 1)
+            if k == 1:
+                prep_cw(0)
             if k == 2:
-                prep_cw_low()
-            if k == 3:
-                prep_cw_high(0, False)
+                prep_cw(1)
                 prep_bias()
-            if k == 4:
-                prep_cw_high(1, True)
-                quantise_cw(1)
             if k + ZBUFS < NB:
                 load_z(k + ZBUFS)
-            if k - LAG_T >= 0 and k - LAG_T + CBUFS < NB:
-                load_c(k - LAG_T + CBUFS)
+            if k - 1 + CBUFS < NB:
+                load_c(k - 1 + CBUFS)
 
-        first = NB - LAG_T - LAG_X
-        for b in range(first, first + FILL):
+        for b in range(NB - 1 - LAG_X, NB - 1):
             s_2(b)
-        e_x_scalar(pending, 0)
-        store(pending)
-        t_oh(NB - 1)
-        for b in range(first, first + FILL):
-            e_x(b)
-        for b in range(first + FILL, NB - 1):
-            s_2(b)
-        q_o(NB - 1)
-        for b in range(first + FILL, NB - 1):
+        e_x(pending)
+        for b in range(NB - 1 - LAG_X, NB - 1):
             e_x(b)
         s_2(NB - 1)
         e_x(NB - 1)

@@ -18,12 +18,14 @@ K = 1024
 O = 512
 BATCH = 256
 NB = TOKENS // BATCH
-LAG_X = 1
+LAG_T = 2
+LAG_X = 2
+FILL = 1
 ZBUFS = 10
 CBUFS = 10
 
 FLOPS = 2 * TOKENS * (512 * 1024 + 256 * 512 + 1024 * 512)
-BYTES = 3 * TOKENS * 1024 * 2 + 2 * (512 * 1024 + 256 * 512) * 2 + O * K * 2 + O * 2
+BYTES = 3 * TOKENS * 1024 * 2 + 2 * (128 * (640 + 768 + 896 + 1024) + 256 * 256) * 2 + O * K * 2 + O * 2
 
 
 def tile_cp_sparse_degree_lu_pb_t_kernel(tc, z, chain_lo, U_hi, masks_hi, C_w, C_b, out):
@@ -40,8 +42,13 @@ def tile_cp_sparse_degree_lu_pb_t_kernel(tc, z, chain_lo, U_hi, masks_hi, C_w, C
         def bank_f32():
             return psum.tile([P, 512], F32, name="bank", tag="bank")
 
+        def bank_bf16():
+            return psum.tile([P, 1024], BF16, name="bankb", tag="bank")
+
         ident_f = keep.tile([P, P], F32, name="ident_f")
+        ident_b = keep.tile([P, P], BF16, name="ident_b")
         make_identity(nc, ident_f[:])
+        make_identity(nc, ident_b[:])
         ones = keep.tile([P, P], BF16, name="ones")
         brow = keep.tile([P, O], BF16, name="brow")
         bias = keep.tile([P, O], F32, name="bias")
@@ -73,43 +80,56 @@ def tile_cp_sparse_degree_lu_pb_t_kernel(tc, z, chain_lo, U_hi, masks_hi, C_w, C
             zn[b] = stream.tile([P, 2 * D], BF16, name="zn", tag="zn", bufs=ZBUFS)
             nc.sync.dma_start(out=zn[b][:].rearrange("p (s c) -> p s c", s=2), in_=rows(zf, b))
 
-        def load_c(b):
-            cn[b] = stream.tile([P, 2 * K], BF16, name="cn", tag="cn", bufs=CBUFS)
-            nc.sync.dma_start(out=cn[b][:].rearrange("p (s c) -> p s c", s=2), in_=rows(chain_lo, b))
+        def load_c(b, lo=0, hi=K):
+            if b not in cn:
+                cn[b] = stream.tile([P, 2 * K], BF16, name="cn", tag="cn", bufs=CBUFS)
+            nc.sync.dma_start(out=cn[b][:].rearrange("p (s c) -> p s c", s=2)[:, :, lo:hi],
+                              in_=rows(chain_lo, b)[:, :, lo:hi])
+
+        def live_w2(t):
+            return 640 + 128 * t
 
         def load_w2(t):
-            kind, par = divmod(t, 2)
-            for dst, src in ((un, U_hi), (mn, masks_hi)):
-                nc.sync.dma_start(out=dst[:, t * D:(t + 1) * D],
-                                  in_=src[0, 256 * kind:256 * kind + 256, :].rearrange("(m e) c -> m e c", e=2)[:, par, :])
+            w = live_w2(t)
+            nc.sync.dma_start(out=un[:, t * D:t * D + w], in_=U_hi[0, t * P:(t + 1) * P, 0:w])
+            nc.sync.dma_start(out=mn[:, t * D:t * D + w], in_=masks_hi[0, t * P:(t + 1) * P, 0:w])
+
+        for t in range(3):
+            nc.vector.memset(un[:, t * D + live_w2(t):(t + 1) * D], 0.0)
+        u33 = u3[:].rearrange("p (t c) -> p t c", t=2)
+        m33 = m3[:].rearrange("p (t c) -> p t c", t=2)
+        nc.vector.memset(u33[:, :, 0:256], 0.0)
 
         load_w2(0)
         load_w2(1)
         load_z(0)
         load_w2(2)
         load_w2(3)
-        nc.sync.dma_start(out=u3[:].rearrange("p (e c) -> p e c", e=2),
-                          in_=U_hi[1, 256:512, 512:1024].rearrange("(m e) c -> m e c", e=2))
-        nc.sync.dma_start(out=m3[:].rearrange("p (e c) -> p e c", e=2),
-                          in_=masks_hi[1, 256:512, 512:1024].rearrange("(m e) c -> m e c", e=2))
-        load_c(0)
+        nc.sync.dma_start(out=u33[:, :, 256:512],
+                          in_=U_hi[1, 256:512, 768:1024].rearrange("(t p) c -> p t c", p=P))
+        nc.sync.dma_start(out=m33[:, :, 256:512],
+                          in_=masks_hi[1, 256:512, 768:1024].rearrange("(t p) c -> p t c", p=P))
         load_z(1)
-        load_c(1)
+        load_c(0, 512, K)
         load_z(2)
+        load_c(0, 0, 512)
+        load_c(1)
+        load_z(3)
         nc.sync.dma_start(out=cwn[:].rearrange("p (t c) -> p t c", t=4),
                           in_=C_w.rearrange("(t p) c -> p t c", p=P))
         nc.sync.dma_start(out=brow[0:1, :], in_=C_b.unsqueeze(0))
         for b in range(2, CBUFS):
             load_c(b)
-            if b + 1 < ZBUFS:
-                load_z(b + 1)
+            if b + 2 < ZBUFS:
+                load_z(b + 2)
 
         unw = un[:].bitcast(F32)
         w2gw = w2g[:].bitcast(F32).rearrange("p (g r u) -> p g r u", g=2, u=2)
 
         def mask_w2(t):
-            nc.vector.tensor_tensor(out=un[:, t * D:(t + 1) * D], in0=un[:, t * D:(t + 1) * D],
-                                    in1=mn[:, t * D:(t + 1) * D], op=MULT)
+            w = live_w2(t)
+            nc.vector.tensor_tensor(out=un[:, t * D:t * D + w], in0=un[:, t * D:t * D + w],
+                                    in1=mn[:, t * D:t * D + w], op=MULT)
 
         def transpose_w2(t):
             bank = bank_f32()
@@ -126,7 +146,7 @@ def tile_cp_sparse_degree_lu_pb_t_kernel(tc, z, chain_lo, U_hi, masks_hi, C_w, C
                                       in_=w2g[:, 4 * c0:4 * c0 + 1024])
 
         def prep_w3():
-            nc.vector.tensor_tensor(out=u3[:], in0=u3[:], in1=m3[:], op=MULT)
+            nc.vector.tensor_tensor(out=u33[:, :, 256:512], in0=u33[:, :, 256:512], in1=m33[:, :, 256:512], op=MULT)
             u3w = u3[:].bitcast(F32)
             bank = bank_f32()
             for u in range(2):
@@ -142,22 +162,36 @@ def tile_cp_sparse_degree_lu_pb_t_kernel(tc, z, chain_lo, U_hi, masks_hi, C_w, C
 
         cww = cwn[:].bitcast(F32)
         cwgw = cwg[:].bitcast(F32).rearrange("p (g r u) -> p g r u", g=2, u=2)
+        cwgb = cwg[:].rearrange("p (g r t) -> p g r t", g=2, t=4)
 
         def quantise_cw(g):
             nc.vector.quantize_mx(out=cwc[:, 512 * g:512 * g + 512].bitcast(FP8X4),
                                   scales=cws[:, 512 * g:512 * g + 512], in_=cwg[:, 2048 * g:2048 * g + 2048])
 
-        def prep_cw(g):
+        def prep_cw_low():
             for h in range(2):
                 bank = bank_f32()
                 for u in range(2):
                     for tl in range(2):
-                        w0 = (2 * h + tl) * 512 + 256 * g + 128 * u
+                        w0 = (2 * h + tl) * 512 + 128 * u
                         nc.tensor.transpose(bank[:, 256 * u + 128 * tl:256 * u + 128 * tl + 128],
                                             cww[:, w0:w0 + 128], ident_f[:])
-                nc.scalar.copy(out=cwgw[:, g, 256 * h:256 * h + 256, :],
+                nc.scalar.copy(out=cwgw[:, 0, 256 * h:256 * h + 256, :],
                                in_=bank[:].rearrange("p (u r) -> p r u", u=2))
-            quantise_cw(g)
+            quantise_cw(0)
+
+        def prep_cw_high(h, on_vector):
+            bankb = bank_bf16()
+            for t in range(4):
+                for tl in range(2):
+                    c0 = (2 * h + tl) * K + 512 + 128 * t
+                    nc.tensor.transpose(bankb[:, 256 * t + 128 * tl:256 * t + 128 * tl + 128],
+                                        cwn[:, c0:c0 + 128], ident_b[:])
+            src = bankb[:].rearrange("p (t r) -> p r t", t=4)
+            if on_vector:
+                nc.vector.tensor_copy(out=cwgb[:, 1, 256 * h:256 * h + 256, :], in_=src)
+            else:
+                nc.scalar.copy(out=cwgb[:, 1, 256 * h:256 * h + 256, :], in_=src)
 
         def prep_bias():
             bb = bank_f32()
@@ -169,6 +203,7 @@ def tile_cp_sparse_degree_lu_pb_t_kernel(tc, z, chain_lo, U_hi, masks_hi, C_w, C
         zs = {}
         y2 = {}
         y3 = {}
+        oh = {}
         og = {}
         oc = {}
         osc = {}
@@ -177,64 +212,74 @@ def tile_cp_sparse_degree_lu_pb_t_kernel(tc, z, chain_lo, U_hi, masks_hi, C_w, C
         def t_z(b):
             zw = zn[b][:].bitcast(F32)
             zg[b] = stream.tile([P, 2048], BF16, name="zg", tag="zg", bufs=2, align_bytes=64)
-            zgw = zg[b][:].bitcast(F32).rearrange("p (g s r u) -> p g s r u", g=2, s=2, u=2)
+            zgw = zg[b][:].bitcast(F32).rearrange("p (s g r u) -> p s g r u", s=2, g=2, u=2)
             for s in range(2):
                 bank = bank_f32()
                 for gu in range(4):
                     nc.tensor.transpose(bank[:, 128 * gu:128 * gu + 128],
                                         zw[:, 512 * s + 128 * gu:512 * s + 128 * gu + 128], ident_f[:])
-                nc.scalar.copy(out=zgw[:, :, s], in_=bank[:].rearrange("p (g u r) -> p g r u", g=2, u=2))
+                nc.scalar.copy(out=zgw[:, s], in_=bank[:].rearrange("p (g u r) -> p g r u", g=2, u=2))
 
         def q_z(b):
             zc[b] = stream.tile([P, 512], U32, name="zc", tag="zc", bufs=2, align_bytes=64)
             zs[b] = stream.tile([P, 512], U8, name="zs", tag="zs", bufs=2, align_bytes=64)
             nc.vector.quantize_mx(out=zc[b][:].bitcast(FP8X4), scales=zs[b][:], in_=zg[b][:])
 
-        def t_c(b):
-            cw_ = cn[b][:].bitcast(F32)
-            og[b] = stream.tile([P, 2048], BF16, name="og", tag="og", bufs=3, align_bytes=64)
-            ogw = og[b][:].bitcast(F32).rearrange("p (g t u) -> p g t u", g=2, u=2)
-            for g in range(2):
-                bank = bank_f32()
-                for u in range(2):
-                    for s in range(2):
-                        w0 = 512 * s + 256 * g + 128 * u
-                        nc.tensor.transpose(bank[:, 256 * u + 128 * s:256 * u + 128 * s + 128],
-                                            cw_[:, w0:w0 + 128], ident_f[:])
-                nc.scalar.copy(out=ogw[:, g], in_=bank[:].rearrange("p (u t) -> p t u", u=2))
-
         def s_1(b):
-            for kind in range(2):
-                y2[(b, kind)] = bank_f32()
-                for e in range(2):
+            for half in range(2):
+                y2[(b, half)] = bank_f32()
+                for s in range(2):
                     for g in range(2):
-                        w0 = 512 * g + 128 * (2 * kind + e)
-                        nc.tensor.matmul_mx(out=y2[(b, kind)][:, 256 * e:256 * e + 256],
-                                            lhsT=w2c[:, w0:w0 + 128].bitcast(FP8X4), lhsT_scale=w2s[:, w0:w0 + 128],
-                                            rhs=zc[b][:, 256 * g:256 * g + 256].bitcast(FP8X4),
-                                            rhs_scale=zs[b][:, 256 * g:256 * g + 256],
+                        c0 = (2 * s + g) * 128
+                        r0 = 512 * g + 256 * half
+                        nc.tensor.matmul_mx(out=y2[(b, half)][:, 256 * s:256 * s + 256],
+                                            lhsT=zc[b][:, c0:c0 + 128].bitcast(FP8X4),
+                                            lhsT_scale=zs[b][:, c0:c0 + 128],
+                                            rhs=w2c[:, r0:r0 + 256].bitcast(FP8X4), rhs_scale=w2s[:, r0:r0 + 256],
                                             start=(g == 0), stop=(g == 1))
             y3[b] = bank_f32()
-            for e in range(2):
-                nc.tensor.matmul_mx(out=y3[b][:, 256 * e:256 * e + 256],
-                                    lhsT=w3c[:, 128 * e:128 * e + 128].bitcast(FP8X4),
-                                    lhsT_scale=w3s[:, 128 * e:128 * e + 128],
-                                    rhs=zc[b][:, 256:512].bitcast(FP8X4), rhs_scale=zs[b][:, 256:512],
+            for s in range(2):
+                c0 = (2 * s + 1) * 128
+                nc.tensor.matmul_mx(out=y3[b][:, 256 * s:256 * s + 256],
+                                    lhsT=zc[b][:, c0:c0 + 128].bitcast(FP8X4), lhsT_scale=zs[b][:, c0:c0 + 128],
+                                    rhs=w3c[:].bitcast(FP8X4), rhs_scale=w3s[:],
                                     start=True, stop=True)
 
         def chain(b):
+            oh[b] = stream.tile([P, 1024], BF16, name="oh", tag="oh", bufs=LAG_T + 2)
             tmp = stream.tile([P, 512], F32, name="tmp", tag="tmp", bufs=2)
-            tmp3 = tmp[:].rearrange("p (t e) -> p t e", e=2)
-            hi = og[b][:].rearrange("p (g t v) -> p g t v", g=2, v=4)
-            nc.vector.scalar_tensor_tensor(out=hi[:, 1, :, 0:2],
-                                           in0=y2[(b, 0)][:].rearrange("p (e t) -> p t e", e=2), scalar=1.0,
-                                           in1=hi[:, 1, :, 0:2], op0=ADD, op1=MULT)
+            oh3 = oh[b][:].rearrange("p (s r) -> p s r", s=2)
+            tmp3 = tmp[:].rearrange("p (s r) -> p s r", s=2)
+            cn3 = cn[b][:].rearrange("p (s c) -> p s c", s=2)
+            nc.vector.scalar_tensor_tensor(out=oh3[:, :, 0:256],
+                                           in0=y2[(b, 0)][:].rearrange("p (s r) -> p s r", s=2), scalar=1.0,
+                                           in1=cn3[:, :, 512:768], op0=ADD, op1=MULT)
             nc.vector.scalar_tensor_tensor(out=tmp3,
-                                           in0=y2[(b, 1)][:].rearrange("p (e t) -> p t e", e=2), scalar=1.0,
-                                           in1=hi[:, 1, :, 2:4], op0=ADD, op1=MULT)
-            nc.vector.scalar_tensor_tensor(out=hi[:, 1, :, 2:4],
-                                           in0=y3[b][:].rearrange("p (e t) -> p t e", e=2), scalar=1.0,
+                                           in0=y2[(b, 1)][:].rearrange("p (s r) -> p s r", s=2), scalar=1.0,
+                                           in1=cn3[:, :, 768:1024], op0=ADD, op1=MULT)
+            nc.vector.scalar_tensor_tensor(out=oh3[:, :, 256:512],
+                                           in0=y3[b][:].rearrange("p (s r) -> p s r", s=2), scalar=1.0,
                                            in1=tmp3, op0=ADD, op1=MULT)
+
+        def t_c(b):
+            cw_ = cn[b][:].bitcast(F32)
+            og[b] = stream.tile([P, 2048], BF16, name="og", tag="og", bufs=2, align_bytes=64)
+            ogw = og[b][:].bitcast(F32).rearrange("p (s g r u) -> p s g r u", s=2, g=2, u=2)
+            bank = bank_f32()
+            for s in range(2):
+                for u in range(2):
+                    nc.tensor.transpose(bank[:, 256 * s + 128 * u:256 * s + 128 * u + 128],
+                                        cw_[:, 512 * s + 128 * u:512 * s + 128 * u + 128], ident_f[:])
+            nc.scalar.copy(out=ogw[:, :, 0], in_=bank[:].rearrange("p (s u r) -> p s r u", s=2, u=2))
+
+        def t_oh(b):
+            ogb = og[b][:].rearrange("p (s g r t) -> p s g r t", s=2, g=2, t=4)
+            bankb = bank_bf16()
+            for s in range(2):
+                for t in range(4):
+                    nc.tensor.transpose(bankb[:, 512 * s + 128 * t:512 * s + 128 * t + 128],
+                                        oh[b][:, 512 * s + 128 * t:512 * s + 128 * t + 128], ident_b[:])
+            nc.scalar.copy(out=ogb[:, :, 1], in_=bankb[:].rearrange("p (s t r) -> p s r t", s=2, t=4))
 
         def q_o(b):
             oc[b] = stream.tile([P, 512], U32, name="oc", tag="oc", bufs=LAG_X + 2, align_bytes=64)
@@ -245,7 +290,7 @@ def tile_cp_sparse_degree_lu_pb_t_kernel(tc, z, chain_lo, U_hi, masks_hi, C_w, C
             for s in range(2):
                 xp[(b, s)] = bank_f32()
                 for g in range(2):
-                    c0 = 256 * g + 128 * s
+                    c0 = (2 * s + g) * 128
                     nc.tensor.matmul_mx(out=xp[(b, s)][:],
                                         lhsT=oc[b][:, c0:c0 + 128].bitcast(FP8X4), lhsT_scale=osc[b][:, c0:c0 + 128],
                                         rhs=cwc[:, 512 * g:512 * g + 512].bitcast(FP8X4),
@@ -260,8 +305,6 @@ def tile_cp_sparse_degree_lu_pb_t_kernel(tc, z, chain_lo, U_hi, masks_hi, C_w, C
             nc.vector.tensor_tensor(out=xs[b][:, 512 * s:512 * s + 512], in0=xp[(b, s)][:], in1=bias[:], op=ADD)
 
         def e_x_scalar(b, s):
-            if b not in xs:
-                xs[b] = stream.tile([P, 1024], F32, name="xs", tag="xs", bufs=6)
             nc.scalar.copy(out=xs[b][:, 512 * s:512 * s + 512], in_=xp[(b, s)][:])
             nc.gpsimd.tensor_tensor(out=xs[b][:, 512 * s:512 * s + 512], in0=xs[b][:, 512 * s:512 * s + 512],
                                     in1=bias[:], op=ADD)
@@ -288,43 +331,59 @@ def tile_cp_sparse_degree_lu_pb_t_kernel(tc, z, chain_lo, U_hi, masks_hi, C_w, C
         prep_w3()
         quantise_w2(1)
         quantise_w3()
-        t_c(0)
         load_z(ZBUFS)
 
         pending = -1
         for k in range(1, NB + 1):
-            b2 = k - 2 - LAG_X
+            b2 = k - LAG_T - 1 - LAG_X
             if k < NB:
                 t_z(k)
             if pending >= 0:
                 e_x_scalar(pending, 0)
-                e_x_scalar(pending, 1)
                 store(pending)
                 pending = -1
-            if k < NB:
-                t_c(k)
+            if k - LAG_T >= 0:
+                t_c(k - LAG_T)
+                t_oh(k - LAG_T)
+            if k == NB:
+                t_c(NB - 1)
             s_1(k - 1)
+            chain(k - 1)
             if k < NB:
                 q_z(k)
-            chain(k - 1)
             if b2 >= 0:
                 s_2(b2)
+                e_x_vector(b2, 1)
                 pending = b2
-            q_o(k - 1)
-            if k == 1:
-                prep_cw(0)
+            if k - LAG_T >= 0:
+                q_o(k - LAG_T)
             if k == 2:
-                prep_cw(1)
+                prep_cw_low()
+            if k == 3:
+                prep_cw_high(0, False)
                 prep_bias()
+            if k == 4:
+                prep_cw_high(1, True)
+                quantise_cw(1)
             if k + ZBUFS < NB:
                 load_z(k + ZBUFS)
-            if k - 1 + CBUFS < NB:
-                load_c(k - 1 + CBUFS)
+            if k - LAG_T >= 0 and k - LAG_T + CBUFS < NB:
+                load_c(k - LAG_T + CBUFS)
 
-        for b in range(NB - 1 - LAG_X, NB - 1):
+        first = NB - LAG_T - LAG_X
+        for b in range(first, first + FILL):
             s_2(b)
-        e_x(pending)
-        for b in range(NB - 1 - LAG_X, NB - 1):
+        e_x_scalar(pending, 0)
+        store(pending)
+        t_oh(NB - 1)
+        for b in range(first, first + FILL):
+            e_x(b)
+        for b in range(first + FILL, NB - 1):
+            s_2(b)
+        q_o(NB - 1)
+        for b in range(first + FILL, NB - 1):
             e_x(b)
         s_2(NB - 1)
-        e_x(NB - 1)
+        for s in range(2):
+            e_x_vector(NB - 1, s)
+            nc.sync.dma_start(out=rows(xf, NB - 1)[:, s, :], in_=xs[NB - 1][:, 512 * s:512 * s + 512])

@@ -42,13 +42,8 @@ def tile_cp_sparse_degree_lu_pb_t_kernel(tc, z, chain_lo, U_hi, masks_hi, C_w, C
         def bank_f32():
             return psum.tile([P, 512], F32, name="bank", tag="bank")
 
-        def bank_bf16():
-            return psum.tile([P, 1024], BF16, name="bankb", tag="bank")
-
         ident_f = keep.tile([P, P], F32, name="ident_f")
-        ident_b = keep.tile([P, P], BF16, name="ident_b")
         make_identity(nc, ident_f[:])
-        make_identity(nc, ident_b[:])
         ones = keep.tile([P, P], BF16, name="ones")
         brow = keep.tile([P, O], BF16, name="brow")
         bias = keep.tile([P, O], F32, name="bias")
@@ -162,36 +157,23 @@ def tile_cp_sparse_degree_lu_pb_t_kernel(tc, z, chain_lo, U_hi, masks_hi, C_w, C
 
         cww = cwn[:].bitcast(F32)
         cwgw = cwg[:].bitcast(F32).rearrange("p (g r u) -> p g r u", g=2, u=2)
-        cwgb = cwg[:].rearrange("p (g r t) -> p g r t", g=2, t=4)
 
         def quantise_cw(g):
             nc.vector.quantize_mx(out=cwc[:, 512 * g:512 * g + 512].bitcast(FP8X4),
                                   scales=cws[:, 512 * g:512 * g + 512], in_=cwg[:, 2048 * g:2048 * g + 2048])
 
-        def prep_cw_low():
-            for h in range(2):
-                bank = bank_f32()
-                for u in range(2):
-                    for tl in range(2):
-                        w0 = (2 * h + tl) * 512 + 128 * u
-                        nc.tensor.transpose(bank[:, 256 * u + 128 * tl:256 * u + 128 * tl + 128],
-                                            cww[:, w0:w0 + 128], ident_f[:])
-                nc.scalar.copy(out=cwgw[:, 0, 256 * h:256 * h + 256, :],
-                               in_=bank[:].rearrange("p (u r) -> p r u", u=2))
-            quantise_cw(0)
-
-        def prep_cw_high(h, on_vector):
-            bankb = bank_bf16()
-            for t in range(4):
+        def prep_cw(g, h, on_vector):
+            bank = bank_f32()
+            for u in range(2):
                 for tl in range(2):
-                    c0 = (2 * h + tl) * K + 512 + 128 * t
-                    nc.tensor.transpose(bankb[:, 256 * t + 128 * tl:256 * t + 128 * tl + 128],
-                                        cwn[:, c0:c0 + 128], ident_b[:])
-            src = bankb[:].rearrange("p (t r) -> p r t", t=4)
+                    w0 = (2 * h + tl) * 512 + 256 * g + 128 * u
+                    nc.tensor.transpose(bank[:, 256 * u + 128 * tl:256 * u + 128 * tl + 128],
+                                        cww[:, w0:w0 + 128], ident_f[:])
+            src = bank[:].rearrange("p (u r) -> p r u", u=2)
             if on_vector:
-                nc.vector.tensor_copy(out=cwgb[:, 1, 256 * h:256 * h + 256, :], in_=src)
+                nc.vector.tensor_copy(out=cwgw[:, g, 256 * h:256 * h + 256, :], in_=src)
             else:
-                nc.scalar.copy(out=cwgb[:, 1, 256 * h:256 * h + 256, :], in_=src)
+                nc.scalar.copy(out=cwgw[:, g, 256 * h:256 * h + 256, :], in_=src)
 
         def prep_bias():
             bb = bank_f32()
@@ -273,13 +255,14 @@ def tile_cp_sparse_degree_lu_pb_t_kernel(tc, z, chain_lo, U_hi, masks_hi, C_w, C
             nc.scalar.copy(out=ogw[:, :, 0], in_=bank[:].rearrange("p (s u r) -> p s r u", s=2, u=2))
 
         def t_oh(b):
-            ogb = og[b][:].rearrange("p (s g r t) -> p s g r t", s=2, g=2, t=4)
-            bankb = bank_bf16()
+            ohw = oh[b][:].bitcast(F32)
+            ogw = og[b][:].bitcast(F32).rearrange("p (s g r u) -> p s g r u", s=2, g=2, u=2)
+            bank = bank_f32()
             for s in range(2):
-                for t in range(4):
-                    nc.tensor.transpose(bankb[:, 512 * s + 128 * t:512 * s + 128 * t + 128],
-                                        oh[b][:, 512 * s + 128 * t:512 * s + 128 * t + 128], ident_b[:])
-            nc.scalar.copy(out=ogb[:, :, 1], in_=bankb[:].rearrange("p (s t r) -> p s r t", s=2, t=4))
+                for u in range(2):
+                    w0 = 256 * s + 128 * u
+                    nc.tensor.transpose(bank[:, w0:w0 + 128], ohw[:, w0:w0 + 128], ident_f[:])
+            nc.scalar.copy(out=ogw[:, :, 1], in_=bank[:].rearrange("p (s u r) -> p s r u", s=2, u=2))
 
         def q_o(b):
             oc[b] = stream.tile([P, 512], U32, name="oc", tag="oc", bufs=LAG_X + 2, align_bytes=64)
@@ -358,12 +341,14 @@ def tile_cp_sparse_degree_lu_pb_t_kernel(tc, z, chain_lo, U_hi, masks_hi, C_w, C
             if k - LAG_T >= 0:
                 q_o(k - LAG_T)
             if k == 2:
-                prep_cw_low()
+                prep_cw(0, 0, False)
+                prep_cw(0, 1, False)
+                quantise_cw(0)
             if k == 3:
-                prep_cw_high(0, False)
+                prep_cw(1, 0, False)
                 prep_bias()
             if k == 4:
-                prep_cw_high(1, True)
+                prep_cw(1, 1, True)
                 quantise_cw(1)
             if k + ZBUFS < NB:
                 load_z(k + ZBUFS)

@@ -208,7 +208,7 @@ def tile_cp_sparse_degree_lu_pb_t_kernel(tc, z, chain_lo, U_hi, masks_hi, C_w, C
             nc.vector.quantize_mx(out=zc[b][:].bitcast(FP8X4), scales=zs[b][:], in_=zg[b][:])
 
         def s_1(b):
-            for half in range(2):
+            for half in (1, 0):
                 y2[(b, half)] = bank_f32()
                 for s in range(2):
                     for g in range(2):
@@ -233,12 +233,12 @@ def tile_cp_sparse_degree_lu_pb_t_kernel(tc, z, chain_lo, U_hi, masks_hi, C_w, C
             oh3 = oh[b][:].rearrange("p (s r) -> p s r", s=2)
             tmp3 = tmp[:].rearrange("p (s r) -> p s r", s=2)
             cn3 = cn[b][:].rearrange("p (s c) -> p s c", s=2)
-            nc.vector.scalar_tensor_tensor(out=oh3[:, :, 0:256],
-                                           in0=y2[(b, 0)][:].rearrange("p (s r) -> p s r", s=2), scalar=1.0,
-                                           in1=cn3[:, :, 512:768], op0=ADD, op1=MULT)
             nc.vector.scalar_tensor_tensor(out=tmp3,
                                            in0=y2[(b, 1)][:].rearrange("p (s r) -> p s r", s=2), scalar=1.0,
                                            in1=cn3[:, :, 768:1024], op0=ADD, op1=MULT)
+            nc.vector.scalar_tensor_tensor(out=oh3[:, :, 0:256],
+                                           in0=y2[(b, 0)][:].rearrange("p (s r) -> p s r", s=2), scalar=1.0,
+                                           in1=cn3[:, :, 512:768], op0=ADD, op1=MULT)
             nc.vector.scalar_tensor_tensor(out=oh3[:, :, 256:512],
                                            in0=y3[b][:].rearrange("p (s r) -> p s r", s=2), scalar=1.0,
                                            in1=tmp3, op0=ADD, op1=MULT)

@@ -25,7 +25,8 @@ ZBUFS = 10
 CBUFS = 10
 
 FLOPS = 2 * TOKENS * (512 * 1024 + 256 * 512 + 1024 * 512)
-BYTES = 3 * TOKENS * 1024 * 2 + 2 * (128 * (640 + 768 + 896 + 1024) + 256 * 256) * 2 + O * K * 2 + O * 2
+BYTES = (2 * TOKENS * 1024 * 2 + TOKENS * O * 4 + (128 * (640 + 768 + 896 + 1024) + 256 * 256) * 2
+         + (4 * 128 * 128 + 256 * 256) * 2 + O * K * 2 + O * 2)
 
 
 def tile_cp_sparse_degree_lu_pb_t_kernel(tc, z, chain_lo, U_hi, masks_hi, C_w, C_b, out):
@@ -51,7 +52,7 @@ def tile_cp_sparse_degree_lu_pb_t_kernel(tc, z, chain_lo, U_hi, masks_hi, C_w, C
         nc.vector.memset(brow[:], 0.0)
 
         un = keep.tile([P, 4 * D], BF16, name="un")
-        mn = keep.tile([P, 4 * D], BF16, name="mn")
+        m2 = keep.tile([P, 4 * P], BF16, name="m2")
         u3 = keep.tile([P, 2 * 512], BF16, name="u3")
         m3 = keep.tile([P, 2 * 512], BF16, name="m3")
         cwn = keep.tile([P, 4 * K], BF16, name="cwn")
@@ -87,7 +88,12 @@ def tile_cp_sparse_degree_lu_pb_t_kernel(tc, z, chain_lo, U_hi, masks_hi, C_w, C
         def load_w2(t):
             w = live_w2(t)
             nc.sync.dma_start(out=un[:, t * D:t * D + w], in_=U_hi[0, t * P:(t + 1) * P, 0:w])
-            nc.sync.dma_start(out=mn[:, t * D:t * D + w], in_=masks_hi[0, t * P:(t + 1) * P, 0:w])
+
+        def load_m2():
+            step = P * D + P
+            flat = masks_hi.rearrange("i p c -> (i p c)")[512:512 + 4 * step]
+            blocks = flat.rearrange("(t x) -> t x", t=4)[:, 0:P * D].rearrange("t (p c) -> p t c", c=D)
+            nc.sync.dma_start(out=m2[:].rearrange("p (t c) -> p t c", t=4), in_=blocks[:, :, 0:P])
 
         for t in range(3):
             nc.vector.memset(un[:, t * D + live_w2(t):(t + 1) * D], 0.0)
@@ -96,6 +102,7 @@ def tile_cp_sparse_degree_lu_pb_t_kernel(tc, z, chain_lo, U_hi, masks_hi, C_w, C
         nc.vector.memset(u33[:, :, 0:256], 0.0)
 
         load_w2(0)
+        load_m2()
         load_w2(1)
         load_z(0)
         load_w2(2)
@@ -122,9 +129,8 @@ def tile_cp_sparse_degree_lu_pb_t_kernel(tc, z, chain_lo, U_hi, masks_hi, C_w, C
         w2gw = w2g[:].bitcast(F32).rearrange("p (g r u) -> p g r u", g=2, u=2)
 
         def mask_w2(t):
-            w = live_w2(t)
-            nc.vector.tensor_tensor(out=un[:, t * D:t * D + w], in0=un[:, t * D:t * D + w],
-                                    in1=mn[:, t * D:t * D + w], op=MULT)
+            diag = un[:, t * D + 512 + 128 * t:t * D + live_w2(t)]
+            nc.vector.tensor_tensor(out=diag, in0=diag, in1=m2[:, 128 * t:128 * t + 128], op=MULT)
 
         def transpose_w2(t):
             bank = bank_f32()
@@ -270,7 +276,7 @@ def tile_cp_sparse_degree_lu_pb_t_kernel(tc, z, chain_lo, U_hi, masks_hi, C_w, C
             nc.vector.quantize_mx(out=oc[b][:].bitcast(FP8X4), scales=osc[b][:], in_=og[b][:])
 
         def s_2(b):
-            for s in range(2):
+            for s in (1, 0):
                 xp[(b, s)] = bank_f32()
                 for g in range(2):
                     c0 = (2 * s + g) * 128

@@ -20,7 +20,6 @@ BATCH = 256
 NB = TOKENS // BATCH
 LAG_T = 2
 LAG_X = 2
-FILL = 1
 ZBUFS = 10
 CBUFS = 10
 
@@ -234,7 +233,7 @@ def tile_cp_sparse_degree_lu_pb_t_kernel(tc, z, chain_lo, U_hi, masks_hi, C_w, C
                                     start=True, stop=True)
 
         def chain(b):
-            oh[b] = stream.tile([P, 1024], BF16, name="oh", tag="oh", bufs=LAG_T + 2)
+            oh[b] = stream.tile([P, 1024], BF16, name="oh", tag="oh", bufs=LAG_T + 3)
             tmp = stream.tile([P, 512], F32, name="tmp", tag="tmp", bufs=2)
             oh3 = oh[b][:].rearrange("p (s r) -> p s r", s=2)
             tmp3 = tmp[:].rearrange("p (s r) -> p s r", s=2)
@@ -251,7 +250,7 @@ def tile_cp_sparse_degree_lu_pb_t_kernel(tc, z, chain_lo, U_hi, masks_hi, C_w, C
 
         def t_c(b):
             cw_ = cn[b][:].bitcast(F32)
-            og[b] = stream.tile([P, 2048], BF16, name="og", tag="og", bufs=2, align_bytes=64)
+            og[b] = stream.tile([P, 2048], BF16, name="og", tag="og", bufs=3, align_bytes=64)
             ogw = og[b][:].bitcast(F32).rearrange("p (s g r u) -> p s g r u", s=2, g=2, u=2)
             bank = bank_f32()
             for s in range(2):
@@ -301,10 +300,8 @@ def tile_cp_sparse_degree_lu_pb_t_kernel(tc, z, chain_lo, U_hi, masks_hi, C_w, C
         def store(b):
             nc.sync.dma_start(out=rows(xf, b), in_=xs[b][:].rearrange("p (s o) -> p s o", s=2))
 
-        def e_x(b):
-            e_x_vector(b, 0)
-            e_x_vector(b, 1)
-            store(b)
+        def store_step(b, s):
+            nc.sync.dma_start(out=rows(xf, b)[:, s, :], in_=xs[b][:, 512 * s:512 * s + 512])
 
         mask_w2(0)
         transpose_w2(0)
@@ -312,69 +309,84 @@ def tile_cp_sparse_degree_lu_pb_t_kernel(tc, z, chain_lo, U_hi, masks_hi, C_w, C
         transpose_w2(1)
         t_z(0)
         mask_w2(2)
+        mask_w2(3)
         quantise_w2(0)
         transpose_w2(2)
-        mask_w2(3)
         transpose_w2(3)
-        q_z(0)
         prep_w3()
+        q_z(0)
         quantise_w2(1)
         quantise_w3()
         load_z(ZBUFS)
 
         pending = -1
+        turned = 0
         for k in range(1, NB + 1):
             b2 = k - LAG_T - 1 - LAG_X
             if k < NB:
                 t_z(k)
-            if pending >= 0:
+            if pending >= 0 and k < NB:
                 e_x_scalar(pending, 0)
                 store(pending)
                 pending = -1
-            if k - LAG_T >= 0:
-                t_c(k - LAG_T)
-                t_oh(k - LAG_T)
+            turn = range(turned, max(turned, k - LAG_T + 1 if k > 4 else k - LAG_T))
+            turned = turn.stop
+            for b in turn:
+                t_c(b)
+                t_oh(b)
             if k == NB:
                 t_c(NB - 1)
+                e_x_scalar(pending, 0)
+                store(pending)
+            if k <= 4:
+                q_z(k)
             s_1(k - 1)
             chain(k - 1)
-            if k < NB:
+            if 4 < k < NB:
                 q_z(k)
             if b2 >= 0:
                 s_2(b2)
                 e_x_vector(b2, 1)
                 pending = b2
-            if k - LAG_T >= 0:
-                q_o(k - LAG_T)
-            if k == 2:
+            for b in turn:
+                q_o(b)
+            if k == 3:
                 prep_cw(0, 0, False)
                 prep_cw(0, 1, False)
                 quantise_cw(0)
-            if k == 3:
-                prep_cw(1, 0, False)
                 prep_bias()
             if k == 4:
+                prep_cw(1, 0, False)
                 prep_cw(1, 1, True)
                 quantise_cw(1)
             if k + ZBUFS < NB:
                 load_z(k + ZBUFS)
-            if k - LAG_T >= 0 and k - LAG_T + CBUFS < NB:
-                load_c(k - LAG_T + CBUFS)
+            for b in turn:
+                if b + CBUFS < NB:
+                    load_c(b + CBUFS)
 
         first = NB - LAG_T - LAG_X
-        for b in range(first, first + FILL):
-            s_2(b)
-        e_x_scalar(pending, 0)
-        store(pending)
+        store_step(first - 1, 1)
+        s_2(first)
         t_oh(NB - 1)
-        for b in range(first, first + FILL):
-            e_x(b)
-        for b in range(first + FILL, NB - 1):
-            s_2(b)
+        e_x_vector(first - 1, 0)
+        store_step(first - 1, 0)
+        e_x_vector(first, 1)
+        store_step(first, 1)
         q_o(NB - 1)
-        for b in range(first + FILL, NB - 1):
-            e_x(b)
+        e_x_scalar(first, 0)
+        s_2(first + 1)
+        e_x_vector(first + 1, 1)
+        store_step(first + 1, 1)
+        e_x_scalar(first + 1, 0)
+        s_2(NB - 2)
+        store_step(first, 0)
+        e_x_vector(NB - 2, 1)
+        store_step(NB - 2, 1)
+        e_x_vector(NB - 2, 0)
+        store_step(NB - 2, 0)
+        store_step(first + 1, 0)
         s_2(NB - 1)
-        for s in range(2):
+        for s in (1, 0):
             e_x_vector(NB - 1, s)
-            nc.sync.dma_start(out=rows(xf, NB - 1)[:, s, :], in_=xs[NB - 1][:, 512 * s:512 * s + 512])
+            store_step(NB - 1, s)

@@ -24,8 +24,8 @@ ZBUFS = 10
 CBUFS = 10
 
 FLOPS = 2 * TOKENS * (512 * 1024 + 256 * 512 + 1024 * 512)
-BYTES = (2 * TOKENS * 1024 * 2 + TOKENS * O * 4 + (128 * (640 + 768 + 896 + 1024) + 256 * 256) * 2
-         + (4 * 128 * 128 + 256 * 256) * 2 + O * K * 2 + O * 2)
+BYTES = (2 * TOKENS * 1024 * 2 + TOKENS * O * 4 + (128 * (640 + 768 + 896 + 1024) + 128 * (256 + 128)) * 2
+         + 2 * 128 * 128 * 2 + O * K * 2 + O * 2)
 
 
 def tile_cp_sparse_degree_lu_pb_t_kernel(tc, z, chain_lo, U_hi, masks_hi, C_w, C_b, out):
@@ -51,19 +51,19 @@ def tile_cp_sparse_degree_lu_pb_t_kernel(tc, z, chain_lo, U_hi, masks_hi, C_w, C
         nc.vector.memset(brow[:], 0.0)
 
         un = keep.tile([P, 4 * D], BF16, name="un")
-        m2 = keep.tile([P, 4 * P], BF16, name="m2")
+        mlow = keep.tile([P, P], BF16, name="mlow")
+        mup = keep.tile([P, P], BF16, name="mup")
         u3 = keep.tile([P, 2 * 512], BF16, name="u3")
-        m3 = keep.tile([P, 2 * 512], BF16, name="m3")
         cwn = keep.tile([P, 4 * K], BF16, name="cwn")
-        w2g = keep.tile([P, 2 * 512 * 4], BF16, name="w2g", align_bytes=64)
-        w3g = keep.tile([P, 256 * 4], BF16, name="w3g", align_bytes=64)
-        cwg = keep.tile([P, 2 * 512 * 4], BF16, name="cwg", align_bytes=64)
-        w2c = keep.tile([P, 2 * 512], U32, name="w2c", align_bytes=64)
-        w2s = keep.tile([P, 2 * 512], U8, name="w2s", align_bytes=64)
-        w3c = keep.tile([P, 256], U32, name="w3c", align_bytes=64)
-        w3s = keep.tile([P, 256], U8, name="w3s", align_bytes=64)
-        cwc = keep.tile([P, 2 * 512], U32, name="cwc", align_bytes=64)
-        cws = keep.tile([P, 2 * 512], U8, name="cws", align_bytes=64)
+        w2g = keep.tile([P, 2 * 512 * 4], BF16, name="w2g", align_bytes=256)
+        w3g = keep.tile([P, 256 * 4], BF16, name="w3g", align_bytes=256)
+        cwg = keep.tile([P, 2 * 512 * 4], BF16, name="cwg", align_bytes=256)
+        w2c = keep.tile([P, 2 * 512], U32, name="w2c", align_bytes=256)
+        w2s = keep.tile([P, 2 * 512], U8, name="w2s", align_bytes=256)
+        w3c = keep.tile([P, 256], U32, name="w3c", align_bytes=256)
+        w3s = keep.tile([P, 256], U8, name="w3s", align_bytes=256)
+        cwc = keep.tile([P, 2 * 512], U32, name="cwc", align_bytes=256)
+        cws = keep.tile([P, 2 * 512], U8, name="cws", align_bytes=256)
 
         zn = {}
         cn = {}
@@ -88,28 +88,21 @@ def tile_cp_sparse_degree_lu_pb_t_kernel(tc, z, chain_lo, U_hi, masks_hi, C_w, C
             w = live_w2(t)
             nc.sync.dma_start(out=un[:, t * D:t * D + w], in_=U_hi[0, t * P:(t + 1) * P, 0:w])
 
-        def load_m2():
-            step = P * D + P
-            flat = masks_hi.rearrange("i p c -> (i p c)")[512:512 + 4 * step]
-            blocks = flat.rearrange("(t x) -> t x", t=4)[:, 0:P * D].rearrange("t (p c) -> p t c", c=D)
-            nc.sync.dma_start(out=m2[:].rearrange("p (t c) -> p t c", t=4), in_=blocks[:, :, 0:P])
-
         for t in range(3):
             nc.vector.memset(un[:, t * D + live_w2(t):(t + 1) * D], 0.0)
         u33 = u3[:].rearrange("p (t c) -> p t c", t=2)
-        m33 = m3[:].rearrange("p (t c) -> p t c", t=2)
         nc.vector.memset(u33[:, :, 0:256], 0.0)
+        nc.vector.memset(u33[:, 1, 256:384], 0.0)
 
+        nc.sync.dma_start(out=mlow[:], in_=masks_hi[0, 0:P, 512:512 + P])
         load_w2(0)
-        load_m2()
         load_w2(1)
         load_z(0)
         load_w2(2)
         load_w2(3)
-        nc.sync.dma_start(out=u33[:, :, 256:512],
-                          in_=U_hi[1, 256:512, 768:1024].rearrange("(t p) c -> p t c", p=P))
-        nc.sync.dma_start(out=m33[:, :, 256:512],
-                          in_=masks_hi[1, 256:512, 768:1024].rearrange("(t p) c -> p t c", p=P))
+        nc.sync.dma_start(out=mup[:], in_=masks_hi[1, 256:256 + P, 768:768 + P])
+        nc.sync.dma_start(out=u33[:, 0, 256:512], in_=U_hi[1, 256:384, 768:1024])
+        nc.sync.dma_start(out=u33[:, 1, 384:512], in_=U_hi[1, 384:512, 896:1024])
         load_z(1)
         load_c(0, 512, K)
         load_z(2)
@@ -129,7 +122,7 @@ def tile_cp_sparse_degree_lu_pb_t_kernel(tc, z, chain_lo, U_hi, masks_hi, C_w, C
 
         def mask_w2(t):
             diag = un[:, t * D + 512 + 128 * t:t * D + live_w2(t)]
-            nc.vector.tensor_tensor(out=diag, in0=diag, in1=m2[:, 128 * t:128 * t + 128], op=MULT)
+            nc.vector.tensor_tensor(out=diag, in0=diag, in1=mlow[:], op=MULT)
 
         def transpose_w2(t):
             bank = bank_f32()
@@ -146,7 +139,9 @@ def tile_cp_sparse_degree_lu_pb_t_kernel(tc, z, chain_lo, U_hi, masks_hi, C_w, C
                                       in_=w2g[:, 4 * c0:4 * c0 + 1024])
 
         def prep_w3():
-            nc.vector.tensor_tensor(out=u33[:, :, 256:512], in0=u33[:, :, 256:512], in1=m33[:, :, 256:512], op=MULT)
+            for tl in range(2):
+                diag = u33[:, tl, 256 + 128 * tl:384 + 128 * tl]
+                nc.vector.tensor_tensor(out=diag, in0=diag, in1=mup[:], op=MULT)
             u3w = u3[:].bitcast(F32)
             bank = bank_f32()
             for u in range(2):
@@ -198,7 +193,7 @@ def tile_cp_sparse_degree_lu_pb_t_kernel(tc, z, chain_lo, U_hi, masks_hi, C_w, C
 
         def t_z(b):
             zw = zn[b][:].bitcast(F32)
-            zg[b] = stream.tile([P, 2048], BF16, name="zg", tag="zg", bufs=2, align_bytes=64)
+            zg[b] = stream.tile([P, 2048], BF16, name="zg", tag="zg", bufs=2, align_bytes=256)
             zgw = zg[b][:].bitcast(F32).rearrange("p (s g r u) -> p s g r u", s=2, g=2, u=2)
             for s in range(2):
                 bank = bank_f32()
@@ -208,8 +203,8 @@ def tile_cp_sparse_degree_lu_pb_t_kernel(tc, z, chain_lo, U_hi, masks_hi, C_w, C
                 nc.scalar.copy(out=zgw[:, s], in_=bank[:].rearrange("p (g u r) -> p g r u", g=2, u=2))
 
         def q_z(b):
-            zc[b] = stream.tile([P, 512], U32, name="zc", tag="zc", bufs=2, align_bytes=64)
-            zs[b] = stream.tile([P, 512], U8, name="zs", tag="zs", bufs=2, align_bytes=64)
+            zc[b] = stream.tile([P, 512], U32, name="zc", tag="zc", bufs=2, align_bytes=256)
+            zs[b] = stream.tile([P, 512], U8, name="zs", tag="zs", bufs=2, align_bytes=256)
             nc.vector.quantize_mx(out=zc[b][:].bitcast(FP8X4), scales=zs[b][:], in_=zg[b][:])
 
         def s_1(b):
@@ -250,7 +245,7 @@ def tile_cp_sparse_degree_lu_pb_t_kernel(tc, z, chain_lo, U_hi, masks_hi, C_w, C
 
         def t_c(b):
             cw_ = cn[b][:].bitcast(F32)
-            og[b] = stream.tile([P, 2048], BF16, name="og", tag="og", bufs=3, align_bytes=64)
+            og[b] = stream.tile([P, 2048], BF16, name="og", tag="og", bufs=3, align_bytes=256)
             ogw = og[b][:].bitcast(F32).rearrange("p (s g r u) -> p s g r u", s=2, g=2, u=2)
             bank = bank_f32()
             for s in range(2):
@@ -270,8 +265,8 @@ def tile_cp_sparse_degree_lu_pb_t_kernel(tc, z, chain_lo, U_hi, masks_hi, C_w, C
             nc.scalar.copy(out=ogw[:, :, 1], in_=bank[:].rearrange("p (s u r) -> p s r u", s=2, u=2))
 
         def q_o(b):
-            oc[b] = stream.tile([P, 512], U32, name="oc", tag="oc", bufs=LAG_X + 2, align_bytes=64)
-            osc[b] = stream.tile([P, 512], U8, name="osc", tag="osc", bufs=LAG_X + 2, align_bytes=64)
+            oc[b] = stream.tile([P, 512], U32, name="oc", tag="oc", bufs=LAG_X + 2, align_bytes=256)
+            osc[b] = stream.tile([P, 512], U8, name="osc", tag="osc", bufs=LAG_X + 2, align_bytes=256)
             nc.vector.quantize_mx(out=oc[b][:].bitcast(FP8X4), scales=osc[b][:], in_=og[b][:])
 
         def s_2(b):
@@ -299,9 +294,6 @@ def tile_cp_sparse_degree_lu_pb_t_kernel(tc, z, chain_lo, U_hi, masks_hi, C_w, C
 
         def store(b):
             nc.sync.dma_start(out=rows(xf, b), in_=xs[b][:].rearrange("p (s o) -> p s o", s=2))
-
-        def store_step(b, s):
-            nc.sync.dma_start(out=rows(xf, b)[:, s, :], in_=xs[b][:, 512 * s:512 * s + 512])
 
         mask_w2(0)
         transpose_w2(0)
@@ -366,27 +358,23 @@ def tile_cp_sparse_degree_lu_pb_t_kernel(tc, z, chain_lo, U_hi, masks_hi, C_w, C
                     load_c(b + CBUFS)
 
         first = NB - LAG_T - LAG_X
-        store_step(first - 1, 1)
         s_2(first)
         t_oh(NB - 1)
         e_x_vector(first - 1, 0)
-        store_step(first - 1, 0)
+        store(first - 1)
         e_x_vector(first, 1)
-        store_step(first, 1)
         q_o(NB - 1)
         e_x_scalar(first, 0)
+        store(first)
         s_2(first + 1)
         e_x_vector(first + 1, 1)
-        store_step(first + 1, 1)
         e_x_scalar(first + 1, 0)
+        store(first + 1)
         s_2(NB - 2)
-        store_step(first, 0)
         e_x_vector(NB - 2, 1)
-        store_step(NB - 2, 1)
         e_x_vector(NB - 2, 0)
-        store_step(NB - 2, 0)
-        store_step(first + 1, 0)
+        store(NB - 2)
         s_2(NB - 1)
         for s in (1, 0):
             e_x_vector(NB - 1, s)
-            store_step(NB - 1, s)
+            nc.sync.dma_start(out=rows(xf, NB - 1)[:, s, :], in_=xs[NB - 1][:, 512 * s:512 * s + 512])

@@ -364,17 +364,15 @@ def tile_cp_sparse_degree_lu_pb_t_kernel(tc, z, chain_lo, U_hi, masks_hi, C_w, C
         store(first - 1)
         e_x_vector(first, 1)
         q_o(NB - 1)
-        e_x_scalar(first, 0)
+        e_x_vector(first, 0)
         store(first)
-        s_2(first + 1)
-        e_x_vector(first + 1, 1)
-        e_x_scalar(first + 1, 0)
-        store(first + 1)
-        s_2(NB - 2)
-        e_x_vector(NB - 2, 1)
-        e_x_vector(NB - 2, 0)
-        store(NB - 2)
-        s_2(NB - 1)
-        for s in (1, 0):
-            e_x_vector(NB - 1, s)
-            nc.sync.dma_start(out=rows(xf, NB - 1)[:, s, :], in_=xs[NB - 1][:, 512 * s:512 * s + 512])
+        for b in range(first + 1, NB):
+            s_2(b)
+            e_x_vector(b, 1)
+            if b == NB - 1:
+                nc.sync.dma_start(out=rows(xf, b)[:, 1, :], in_=xs[b][:, 512:1024])
+            e_x_vector(b, 0)
+            if b == NB - 1:
+                nc.sync.dma_start(out=rows(xf, b)[:, 0, :], in_=xs[b][:, 0:512])
+            else:
+                store(b)

from contextlib import ExitStack

import concourse.mybir as mybir
from concourse.masks import make_identity

F32 = mybir.dt.float32
BF16 = mybir.dt.bfloat16
U32 = mybir.dt.uint32
U8 = mybir.dt.uint8
FP8X4 = mybir.dt.float8_e4m3fn_x4
ADD = mybir.AluOpType.add
MULT = mybir.AluOpType.mult

P = 128
TOKENS = 4096
D = 1024
K = 1024
O = 512
BATCH = 256
NB = TOKENS // BATCH
LAG_T = 2
LAG_X = 2
ZBUFS = 10
CBUFS = 10

FLOPS = 2 * TOKENS * (512 * 1024 + 256 * 512 + 1024 * 512)
BYTES = (2 * TOKENS * 1024 * 2 + TOKENS * O * 4 + (128 * (640 + 768 + 896 + 1024) + 128 * (256 + 128)) * 2
         + 2 * 128 * 128 * 2 + O * K * 2 + O * 2)


def tile_cp_sparse_degree_lu_pb_t_kernel(tc, z, chain_lo, U_hi, masks_hi, C_w, C_b, out):
    nc = tc.nc
    zf = z.flatten_outer_dims()
    xf = out.flatten_outer_dims()

    with ExitStack() as ctx:
        keep = ctx.enter_context(tc.tile_pool(name="keep", bufs=1))
        stream = ctx.enter_context(tc.tile_pool(name="stream", bufs=2))
        psum = ctx.enter_context(tc.psum_pool(name="psum", bufs=8))
        ctx.enter_context(tc.manual_schedule())

        def bank_f32():
            return psum.tile([P, 512], F32, name="bank", tag="bank")

        ident_f = keep.tile([P, P], F32, name="ident_f")
        make_identity(nc, ident_f[:])
        ones = keep.tile([P, P], BF16, name="ones")
        brow = keep.tile([P, O], BF16, name="brow")
        bias = keep.tile([P, O], F32, name="bias")
        nc.vector.memset(ones[:], 1.0)
        nc.vector.memset(brow[:], 0.0)

        un = keep.tile([P, 4 * D], BF16, name="un")
        mlow = keep.tile([P, P], BF16, name="mlow")
        mup = keep.tile([P, P], BF16, name="mup")
        u3 = keep.tile([P, 2 * 512], BF16, name="u3")
        cwn = keep.tile([P, 4 * K], BF16, name="cwn")
        w2g = keep.tile([P, 2 * 512 * 4], BF16, name="w2g", align_bytes=256)
        w3g = keep.tile([P, 256 * 4], BF16, name="w3g", align_bytes=256)
        cwg = keep.tile([P, 2 * 512 * 4], BF16, name="cwg", align_bytes=256)
        w2c = keep.tile([P, 2 * 512], U32, name="w2c", align_bytes=256)
        w2s = keep.tile([P, 2 * 512], U8, name="w2s", align_bytes=256)
        w3c = keep.tile([P, 256], U32, name="w3c", align_bytes=256)
        w3s = keep.tile([P, 256], U8, name="w3s", align_bytes=256)
        cwc = keep.tile([P, 2 * 512], U32, name="cwc", align_bytes=256)
        cws = keep.tile([P, 2 * 512], U8, name="cws", align_bytes=256)

        zn = {}
        cn = {}

        def rows(ap2d, b):
            return ap2d[b * BATCH:(b + 1) * BATCH, :].rearrange("(p s) c -> p s c", s=2)

        def load_z(b):
            zn[b] = stream.tile([P, 2 * D], BF16, name="zn", tag="zn", bufs=ZBUFS)
            nc.sync.dma_start(out=zn[b][:].rearrange("p (s c) -> p s c", s=2), in_=rows(zf, b))

        def load_c(b, lo=0, hi=K):
            if b not in cn:
                cn[b] = stream.tile([P, 2 * K], BF16, name="cn", tag="cn", bufs=CBUFS)
            nc.sync.dma_start(out=cn[b][:].rearrange("p (s c) -> p s c", s=2)[:, :, lo:hi],
                              in_=rows(chain_lo, b)[:, :, lo:hi])

        def live_w2(t):
            return 640 + 128 * t

        def load_w2(t):
            w = live_w2(t)
            nc.sync.dma_start(out=un[:, t * D:t * D + w], in_=U_hi[0, t * P:(t + 1) * P, 0:w])

        for t in range(3):
            nc.vector.memset(un[:, t * D + live_w2(t):(t + 1) * D], 0.0)
        u33 = u3[:].rearrange("p (t c) -> p t c", t=2)
        nc.vector.memset(u33[:, :, 0:256], 0.0)
        nc.vector.memset(u33[:, 1, 256:384], 0.0)

        nc.sync.dma_start(out=mlow[:], in_=masks_hi[0, 0:P, 512:512 + P])
        load_w2(0)
        load_w2(1)
        load_z(0)
        load_w2(2)
        load_w2(3)
        nc.sync.dma_start(out=mup[:], in_=masks_hi[1, 256:256 + P, 768:768 + P])
        nc.sync.dma_start(out=u33[:, 0, 256:512], in_=U_hi[1, 256:384, 768:1024])
        nc.sync.dma_start(out=u33[:, 1, 384:512], in_=U_hi[1, 384:512, 896:1024])
        load_z(1)
        load_c(0, 512, K)
        load_z(2)
        load_c(0, 0, 512)
        load_c(1)
        load_z(3)
        nc.sync.dma_start(out=cwn[:].rearrange("p (t c) -> p t c", t=4),
                          in_=C_w.rearrange("(t p) c -> p t c", p=P))
        nc.sync.dma_start(out=brow[0:1, :], in_=C_b.unsqueeze(0))
        for b in range(2, CBUFS):
            load_c(b)
            if b + 2 < ZBUFS:
                load_z(b + 2)

        unw = un[:].bitcast(F32)
        w2gw = w2g[:].bitcast(F32).rearrange("p (g r u) -> p g r u", g=2, u=2)

        def mask_w2(t):
            diag = un[:, t * D + 512 + 128 * t:t * D + live_w2(t)]
            nc.vector.tensor_tensor(out=diag, in0=diag, in1=mlow[:], op=MULT)

        def transpose_w2(t):
            bank = bank_f32()
            for gu in range(4):
                nc.tensor.transpose(bank[:, 128 * gu:128 * gu + 128],
                                    unw[:, 512 * t + 128 * gu:512 * t + 128 * gu + 128], ident_f[:])
            nc.scalar.copy(out=w2gw[:, :, 128 * t:128 * t + 128, :],
                           in_=bank[:].rearrange("p (g u r) -> p g r u", g=2, u=2))

        def quantise_w2(half):
            for g in range(2):
                c0 = 512 * g + 256 * half
                nc.vector.quantize_mx(out=w2c[:, c0:c0 + 256].bitcast(FP8X4), scales=w2s[:, c0:c0 + 256],
                                      in_=w2g[:, 4 * c0:4 * c0 + 1024])

        def prep_w3():
            for tl in range(2):
                diag = u33[:, tl, 256 + 128 * tl:384 + 128 * tl]
                nc.vector.tensor_tensor(out=diag, in0=diag, in1=mup[:], op=MULT)
            u3w = u3[:].bitcast(F32)
            bank = bank_f32()
            for u in range(2):
                for tl in range(2):
                    w0 = tl * 256 + 128 * u
                    nc.tensor.transpose(bank[:, 256 * u + 128 * tl:256 * u + 128 * tl + 128],
                                        u3w[:, w0:w0 + 128], ident_f[:])
            nc.scalar.copy(out=w3g[:].bitcast(F32).rearrange("p (r u) -> p r u", u=2),
                           in_=bank[:].rearrange("p (u r) -> p r u", u=2))

        def quantise_w3():
            nc.vector.quantize_mx(out=w3c[:].bitcast(FP8X4), scales=w3s[:], in_=w3g[:])

        cww = cwn[:].bitcast(F32)
        cwgw = cwg[:].bitcast(F32).rearrange("p (g r u) -> p g r u", g=2, u=2)

        def quantise_cw(g):
            nc.vector.quantize_mx(out=cwc[:, 512 * g:512 * g + 512].bitcast(FP8X4),
                                  scales=cws[:, 512 * g:512 * g + 512], in_=cwg[:, 2048 * g:2048 * g + 2048])

        def prep_cw(g, h, on_vector):
            bank = bank_f32()
            for u in range(2):
                for tl in range(2):
                    w0 = (2 * h + tl) * 512 + 256 * g + 128 * u
                    nc.tensor.transpose(bank[:, 256 * u + 128 * tl:256 * u + 128 * tl + 128],
                                        cww[:, w0:w0 + 128], ident_f[:])
            src = bank[:].rearrange("p (u r) -> p r u", u=2)
            if on_vector:
                nc.vector.tensor_copy(out=cwgw[:, g, 256 * h:256 * h + 256, :], in_=src)
            else:
                nc.scalar.copy(out=cwgw[:, g, 256 * h:256 * h + 256, :], in_=src)

        def prep_bias():
            bb = bank_f32()
            nc.tensor.matmul(out=bb[:], lhsT=ones[:], rhs=brow[:], start=True, stop=True)
            nc.scalar.copy(out=bias[:], in_=bb[:])

        zg = {}
        zc = {}
        zs = {}
        y2 = {}
        y3 = {}
        oh = {}
        og = {}
        oc = {}
        osc = {}
        xp = {}

        def t_z(b):
            zw = zn[b][:].bitcast(F32)
            zg[b] = stream.tile([P, 2048], BF16, name="zg", tag="zg", bufs=2, align_bytes=256)
            zgw = zg[b][:].bitcast(F32).rearrange("p (s g r u) -> p s g r u", s=2, g=2, u=2)
            for s in range(2):
                bank = bank_f32()
                for gu in range(4):
                    nc.tensor.transpose(bank[:, 128 * gu:128 * gu + 128],
                                        zw[:, 512 * s + 128 * gu:512 * s + 128 * gu + 128], ident_f[:])
                nc.scalar.copy(out=zgw[:, s], in_=bank[:].rearrange("p (g u r) -> p g r u", g=2, u=2))

        def q_z(b):
            zc[b] = stream.tile([P, 512], U32, name="zc", tag="zc", bufs=2, align_bytes=256)
            zs[b] = stream.tile([P, 512], U8, name="zs", tag="zs", bufs=2, align_bytes=256)
            nc.vector.quantize_mx(out=zc[b][:].bitcast(FP8X4), scales=zs[b][:], in_=zg[b][:])

        def s_1(b):
            for half in (1, 0):
                y2[(b, half)] = bank_f32()
                for s in range(2):
                    for g in range(2):
                        c0 = (2 * s + g) * 128
                        r0 = 512 * g + 256 * half
                        nc.tensor.matmul_mx(out=y2[(b, half)][:, 256 * s:256 * s + 256],
                                            lhsT=zc[b][:, c0:c0 + 128].bitcast(FP8X4),
                                            lhsT_scale=zs[b][:, c0:c0 + 128],
                                            rhs=w2c[:, r0:r0 + 256].bitcast(FP8X4), rhs_scale=w2s[:, r0:r0 + 256],
                                            start=(g == 0), stop=(g == 1))
            y3[b] = bank_f32()
            for s in range(2):
                c0 = (2 * s + 1) * 128
                nc.tensor.matmul_mx(out=y3[b][:, 256 * s:256 * s + 256],
                                    lhsT=zc[b][:, c0:c0 + 128].bitcast(FP8X4), lhsT_scale=zs[b][:, c0:c0 + 128],
                                    rhs=w3c[:].bitcast(FP8X4), rhs_scale=w3s[:],
                                    start=True, stop=True)

        def chain(b):
            oh[b] = stream.tile([P, 1024], BF16, name="oh", tag="oh", bufs=LAG_T + 3)
            tmp = stream.tile([P, 512], F32, name="tmp", tag="tmp", bufs=2)
            oh3 = oh[b][:].rearrange("p (s r) -> p s r", s=2)
            tmp3 = tmp[:].rearrange("p (s r) -> p s r", s=2)
            cn3 = cn[b][:].rearrange("p (s c) -> p s c", s=2)
            nc.vector.scalar_tensor_tensor(out=tmp3,
                                           in0=y2[(b, 1)][:].rearrange("p (s r) -> p s r", s=2), scalar=1.0,
                                           in1=cn3[:, :, 768:1024], op0=ADD, op1=MULT)
            nc.vector.scalar_tensor_tensor(out=oh3[:, :, 0:256],
                                           in0=y2[(b, 0)][:].rearrange("p (s r) -> p s r", s=2), scalar=1.0,
                                           in1=cn3[:, :, 512:768], op0=ADD, op1=MULT)
            nc.vector.scalar_tensor_tensor(out=oh3[:, :, 256:512],
                                           in0=y3[b][:].rearrange("p (s r) -> p s r", s=2), scalar=1.0,
                                           in1=tmp3, op0=ADD, op1=MULT)

        def t_c(b):
            cw_ = cn[b][:].bitcast(F32)
            og[b] = stream.tile([P, 2048], BF16, name="og", tag="og", bufs=3, align_bytes=256)
            ogw = og[b][:].bitcast(F32).rearrange("p (s g r u) -> p s g r u", s=2, g=2, u=2)
            bank = bank_f32()
            for s in range(2):
                for u in range(2):
                    nc.tensor.transpose(bank[:, 256 * s + 128 * u:256 * s + 128 * u + 128],
                                        cw_[:, 512 * s + 128 * u:512 * s + 128 * u + 128], ident_f[:])
            nc.scalar.copy(out=ogw[:, :, 0], in_=bank[:].rearrange("p (s u r) -> p s r u", s=2, u=2))

        def t_oh(b):
            ohw = oh[b][:].bitcast(F32)
            ogw = og[b][:].bitcast(F32).rearrange("p (s g r u) -> p s g r u", s=2, g=2, u=2)
            bank = bank_f32()
            for s in range(2):
                for u in range(2):
                    w0 = 256 * s + 128 * u
                    nc.tensor.transpose(bank[:, w0:w0 + 128], ohw[:, w0:w0 + 128], ident_f[:])
            nc.scalar.copy(out=ogw[:, :, 1], in_=bank[:].rearrange("p (s u r) -> p s r u", s=2, u=2))

        def q_o(b):
            oc[b] = stream.tile([P, 512], U32, name="oc", tag="oc", bufs=LAG_X + 2, align_bytes=256)
            osc[b] = stream.tile([P, 512], U8, name="osc", tag="osc", bufs=LAG_X + 2, align_bytes=256)
            nc.vector.quantize_mx(out=oc[b][:].bitcast(FP8X4), scales=osc[b][:], in_=og[b][:])

        def s_2(b):
            for s in (1, 0):
                xp[(b, s)] = bank_f32()
                for g in range(2):
                    c0 = (2 * s + g) * 128
                    nc.tensor.matmul_mx(out=xp[(b, s)][:],
                                        lhsT=oc[b][:, c0:c0 + 128].bitcast(FP8X4), lhsT_scale=osc[b][:, c0:c0 + 128],
                                        rhs=cwc[:, 512 * g:512 * g + 512].bitcast(FP8X4),
                                        rhs_scale=cws[:, 512 * g:512 * g + 512],
                                        start=(g == 0), stop=(g == 1))

        xs = {}

        def e_x_vector(b, s):
            if b not in xs:
                xs[b] = stream.tile([P, 1024], F32, name="xs", tag="xs", bufs=6)
            nc.vector.tensor_tensor(out=xs[b][:, 512 * s:512 * s + 512], in0=xp[(b, s)][:], in1=bias[:], op=ADD)

        def e_x_scalar(b, s):
            nc.scalar.copy(out=xs[b][:, 512 * s:512 * s + 512], in_=xp[(b, s)][:])
            nc.gpsimd.tensor_tensor(out=xs[b][:, 512 * s:512 * s + 512], in0=xs[b][:, 512 * s:512 * s + 512],
                                    in1=bias[:], op=ADD)

        def store(b):
            nc.sync.dma_start(out=rows(xf, b), in_=xs[b][:].rearrange("p (s o) -> p s o", s=2))

        mask_w2(0)
        transpose_w2(0)
        mask_w2(1)
        transpose_w2(1)
        t_z(0)
        mask_w2(2)
        mask_w2(3)
        quantise_w2(0)
        transpose_w2(2)
        transpose_w2(3)
        prep_w3()
        q_z(0)
        quantise_w2(1)
        quantise_w3()
        load_z(ZBUFS)

        pending = -1
        turned = 0
        for k in range(1, NB + 1):
            b2 = k - LAG_T - 1 - LAG_X
            if k < NB:
                t_z(k)
            if pending >= 0 and k < NB:
                e_x_scalar(pending, 0)
                store(pending)
                pending = -1
            turn = range(turned, max(turned, k - LAG_T + 1 if k > 4 else k - LAG_T))
            turned = turn.stop
            for b in turn:
                t_c(b)
                t_oh(b)
            if k == NB:
                t_c(NB - 1)
                e_x_scalar(pending, 0)
                store(pending)
            if k <= 4:
                q_z(k)
            s_1(k - 1)
            chain(k - 1)
            if 4 < k < NB:
                q_z(k)
            if b2 >= 0:
                s_2(b2)
                e_x_vector(b2, 1)
                pending = b2
            for b in turn:
                q_o(b)
            if k == 3:
                prep_cw(0, 0, False)
                prep_cw(0, 1, False)
                quantise_cw(0)
                prep_bias()
            if k == 4:
                prep_cw(1, 0, False)
                prep_cw(1, 1, True)
                quantise_cw(1)
            if k + ZBUFS < NB:
                load_z(k + ZBUFS)
            for b in turn:
                if b + CBUFS < NB:
                    load_c(b + CBUFS)

        first = NB - LAG_T - LAG_X
        s_2(first)
        t_oh(NB - 1)
        e_x_vector(first - 1, 0)
        store(first - 1)
        e_x_vector(first, 1)
        q_o(NB - 1)
        e_x_vector(first, 0)
        store(first)
        for b in range(first + 1, NB):
            s_2(b)
            e_x_vector(b, 1)
            if b == NB - 1:
                nc.sync.dma_start(out=rows(xf, b)[:, 1, :], in_=xs[b][:, 512:1024])
            e_x_vector(b, 0)
            if b == NB - 1:
                nc.sync.dma_start(out=rows(xf, b)[:, 0, :], in_=xs[b][:, 0:512])
            else:
                store(b)
